import numpy as np
import ml_dtypes


def mxq(x, axis, fmt="e4m3"):
    dtype, down = {"e4m3": (ml_dtypes.float8_e4m3fn, 7), "e5m2": (ml_dtypes.float8_e5m2, 14)}[fmt]
    v = np.moveaxis(np.asarray(x, np.float32).astype(ml_dtypes.bfloat16).astype(np.float64), axis, -1)
    blocks = v.reshape(v.shape[:-1] + (-1, 32))
    amax = np.abs(blocks).max(-1, keepdims=True)
    byte = np.maximum(np.where(amax > 0, np.frexp(amax)[1] - 1 + 127, 0) - down, 1)
    scale = np.exp2(byte - 127.0)
    codes = (blocks / scale).astype(np.float32).astype(dtype).astype(np.float64)
    return np.moveaxis((codes * scale).reshape(v.shape), -1, axis)


WIDE = False


def mx_kscale(k):
    if not WIDE:
        return np.ones(k)
    levels = np.array([10, -10, 5, -5, 0])
    a = np.random.permutation(np.resize(levels, k // 512 * 4)).reshape(k // 512, 4)
    idx = np.arange(k)
    return np.exp2(a[idx // 512, idx % 128 // 32])


BF16 = ml_dtypes.bfloat16


def bf(x):
    return np.asarray(x, np.float32).astype(BF16)


def f64(x):
    return np.asarray(x).astype(np.float64)


E2M1 = np.array([0.0, 0.5, 1.0, 1.5, 2.0, 3.0, 4.0, 6.0, -0.0, -0.5, -1.0, -1.5, -2.0, -3.0, -4.0, -6.0])


def pack_weight(w, fmt):
    k, n = w.shape
    w = f64(bf(w)).reshape(k // 32, 32, n)
    amax = np.abs(w).max(1)
    if fmt == "e4m3":
        byte = np.frexp(amax)[1] - 1 + 127 - 7
    else:
        mant, ex = np.frexp(amax / 6.0)
        byte = np.where(mant > 0.5, ex, ex - 1) + 127
    byte = np.clip(np.where(amax > 0, byte, 1), 1, 254)
    scaled = (w * np.exp2(127.0 - byte)[:, None, :]).reshape(k, n).astype(np.float32)
    by_word = np.ascontiguousarray(scaled.reshape(k // 512, 128, 4, n).transpose(0, 1, 3, 2))
    if fmt == "e4m3":
        words = by_word.astype(ml_dtypes.float8_e4m3fn).view(np.uint8)
    else:
        c = by_word.astype(ml_dtypes.float4_e2m1fn).view(np.uint8) & 0xF
        words = c[..., 0::2] | (c[..., 1::2] << 4)
    return np.ascontiguousarray(words), np.ascontiguousarray(byte.astype(np.uint8).reshape(k // 512, 16, n))


def unpack_weight(words, scales, fmt):
    g, p, n, _ = words.shape
    if fmt == "e4m3":
        vals = np.ascontiguousarray(words).view(ml_dtypes.float8_e4m3fn).astype(np.float64)
    else:
        nib = np.empty((g, p, n, 4), np.uint8)
        nib[..., 0::2] = words & 0xF
        nib[..., 1::2] = words >> 4
        vals = E2M1[nib]
    vals = vals * np.repeat(np.exp2(scales.astype(np.float64) - 127.0), 8, axis=1)[..., None]
    return vals.transpose(0, 1, 3, 2).reshape(g * 512, n)

def pack4(w):
    words, scales = pack_weight(w, "e2m1")
    return words.reshape(words.shape[0], 128, -1), scales


def unpack4(words, scales):
    return unpack_weight(words.reshape(words.shape[0], 128, -1, 2), scales, "e2m1")


B, S, HID, NH, NOPE, ROPE, VD, KV_RANK, SW, QB = 1, 8192, 512, 2, 64, 64, 128, 512, 384, 128
QK = NOPE + ROPE


def rotate_half(x):
    h = x.shape[-1] // 2
    return np.concatenate([-x[..., h:], x[..., :h]], axis=-1)


def rope_tables():
    pos = np.arange(S, dtype=np.float64)
    inv = 1.0 / (10000.0 ** (np.arange(0, ROPE, 2, dtype=np.float64) / ROPE))
    ang = pos[:, None] * inv[None, :]
    ang = np.concatenate([ang, ang], axis=-1)
    return bf(np.broadcast_to(np.cos(ang)[None], (B, S, ROPE))), bf(np.broadcast_to(np.sin(ang)[None], (B, S, ROPE)))


def setup_inputs():
    s = mx_kscale(HID)
    cos, sin = rope_tables()
    hidden_states = bf(np.random.standard_normal((B, S, HID)) * s)
    Wq_words, Wq_scales = pack4(np.random.standard_normal((HID, NH * QK)) * 2.0 / np.sqrt(HID) / s[:, None])
    bq = bf(np.random.standard_normal(NH * QK) * 0.2)
    return {"hidden_states": hidden_states, "cos": cos, "sin": sin,
            "Wq_words": Wq_words, "Wq_scales": Wq_scales,
            "bq": bq}


def reference(hidden_states, cos, sin, Wq_words, Wq_scales, bq):
    q = ((mxq(f64(hidden_states), 2, "e4m3") @ unpack4(Wq_words, Wq_scales)) + f64(bq)).reshape(B, S, NH, QK).transpose(0, 2, 1, 3)
    q_nope, q_rope = q[..., :NOPE], q[..., NOPE:]
    c, si = f64(cos)[:, None], f64(sin)[:, None]
    q_rope = q_rope * c + rotate_half(q_rope) * si
    return np.concatenate([q_nope, q_rope], axis=-1)

@@ -1,0 +1,178 @@
+from contextlib import ExitStack
+
+import concourse.mybir as mybir
+from concourse.masks import make_identity
+
+F32 = mybir.dt.float32
+BF16 = mybir.dt.bfloat16
+I32 = mybir.dt.int32
+U32 = mybir.dt.uint32
+U8 = mybir.dt.uint8
+FP8X4 = mybir.dt.float8_e4m3fn_x4
+FP4X4 = mybir.dt.float4_e2m1fn_x4
+ALU = mybir.AluOpType
+
+P = 128
+PACK = 4
+TOKENS = 8192
+HID = 512
+HEADS = 2
+HEAD_DIM = 128
+NOPE = 64
+ROPE = 64
+HALF = ROPE // 2
+FEATURES = HEADS * HEAD_DIM
+ROWS = TOKENS // P
+GROUP = 4
+GROUPS = ROWS // GROUP
+BANK_ROWS = 2
+TABLE_PART = 16
+WORDS = HID // 2
+
+FLOPS = 2 * TOKENS * HID * FEATURES
+
+
+def tile_gptossmlaattention_pb_t_kernel(
+    tc, hidden_states, cos, sin, Wq_words, Wq_scales, bq, out
+):
+    nc = tc.nc
+    x_dram = hidden_states[0].rearrange("(p n) k -> p n k", p=P)
+    cos_dram = cos[0].rearrange("(p n) j -> p n j", p=P)
+    sin_dram = sin[0].rearrange("(p n) j -> p n j", p=P)
+    out_dram = out[0].rearrange("h (p n) d -> p h n d", p=P)
+
+    with ExitStack() as pools:
+        const = pools.enter_context(tc.tile_pool(name="const", bufs=1))
+        x_pool = pools.enter_context(tc.tile_pool(name="x", bufs=GROUPS))
+        mx_pool = pools.enter_context(tc.tile_pool(name="mx", bufs=3))
+        rope_pool = pools.enter_context(tc.tile_pool(name="rope", bufs=2))
+        out_pool = pools.enter_context(tc.tile_pool(name="outs", bufs=4))
+        words_psum = pools.enter_context(tc.psum_pool(name="words", bufs=4))
+        q_psum = pools.enter_context(tc.psum_pool(name="q", bufs=4))
+
+        ident = const.tile([P, P], F32)
+        make_identity(nc, ident[:])
+
+        w_scales = const.tile([P, FEATURES], U8, align_bytes=64)
+        nc.vector.memset(w_scales[:].bitcast(I32), 0)
+        w_words = const.tile([P, 2 * FEATURES], U8, align_bytes=64)
+        bias_bf = const.tile([P, FEATURES], BF16)
+        bias = const.tile([P, FEATURES], F32)
+
+        x_tiles = []
+        cos_parts = []
+        sin_parts = []
+        for g in range(GROUPS):
+            rows = slice(g * GROUP, (g + 1) * GROUP)
+            x_sb = x_pool.tile([P, GROUP, HID], BF16, name="x_sb")
+            nc.sync.dma_start(out=x_sb[:], in_=x_dram[:, rows, :])
+            x_tiles.append(x_sb)
+            if g == 0:
+                nc.sync.dma_start(out=w_words[:].bitcast(I32), in_=Wq_words[0].bitcast(I32))
+                for quad in range(4):
+                    nc.sync.dma_start(
+                        out=w_scales[32 * quad : 32 * quad + 4, :].bitcast(I32),
+                        in_=Wq_scales[0, 4 * quad : 4 * quad + 4, :].bitcast(I32),
+                    )
+                nc.sync.dma_start(out=bias_bf[:], in_=bq.partition_broadcast(P))
+            if (g * GROUP) % TABLE_PART == 0:
+                part = slice(g * GROUP, g * GROUP + TABLE_PART)
+                cos_sb = const.tile([P, TABLE_PART, ROPE], BF16, name="cos%d" % len(cos_parts))
+                sin_sb = const.tile([P, TABLE_PART, ROPE], BF16, name="sin%d" % len(sin_parts))
+                nc.sync.dma_start(out=cos_sb[:], in_=cos_dram[:, part, :])
+                nc.sync.dma_start(out=sin_sb[:], in_=sin_dram[:, part, :])
+                cos_parts.append(cos_sb)
+                sin_parts.append(sin_sb)
+        nc.scalar.copy(out=bias[:], in_=bias_bf[:])
+
+        def transpose_and_quantise(g):
+            x_words = x_tiles[g][:].bitcast(F32)
+            grouped = mx_pool.tile([P, GROUP, P, PACK], BF16, align_bytes=64, name="grouped")
+            grouped_words = grouped[:].bitcast(F32)
+            for first in range(0, GROUP, BANK_ROWS):
+                flipped = words_psum.tile([P, BANK_ROWS, 2, P], F32, name="flipped")
+                for a in range(BANK_ROWS):
+                    for u in range(2):
+                        nc.tensor.transpose(
+                            flipped[:, a, u, :], x_words[:, first + a, u:WORDS:2], ident[:]
+                        )
+                nc.scalar.copy(
+                    out=grouped_words[:, first : first + BANK_ROWS, :, :],
+                    in_=flipped[:].rearrange("p a u r -> p a r u"),
+                )
+            codes = mx_pool.tile([P, GROUP * P], U32, align_bytes=64, name="codes")
+            scales = mx_pool.tile([P, GROUP * P], U8, align_bytes=64, name="scales")
+            nc.vector.quantize_mx(
+                out=codes[:].bitcast(FP8X4),
+                scales=scales[:],
+                in_=grouped[:].rearrange("p a r t -> p (a r t)"),
+            )
+            return codes, scales
+
+        def project_and_rotate(g, codes, scales):
+            q_sb = out_pool.tile([P, HEADS, GROUP, HEAD_DIM], F32, name="q_sb")
+            for first in range(0, GROUP, BANK_ROWS):
+                q_ps = q_psum.tile([P, BANK_ROWS, FEATURES], F32, name="q_ps")
+                for a in range(BANK_ROWS):
+                    tokens = slice((first + a) * P, (first + a + 1) * P)
+                    nc.tensor.matmul_mx(
+                        out=q_ps[:, a, :],
+                        lhsT=codes[:, tokens].bitcast(FP8X4),
+                        lhsT_scale=scales[:, tokens],
+                        rhs=w_words[:].bitcast(FP4X4),
+                        rhs_scale=w_scales[:],
+                        start=True,
+                        stop=True,
+                    )
+                nc.vector.tensor_tensor(
+                    out=q_sb[:, :, first : first + BANK_ROWS, :].rearrange("p h a d -> p a h d"),
+                    in0=q_ps[:].rearrange("p a (h d) -> p a h d", h=HEADS),
+                    in1=bias[:]
+                    .rearrange("p (h d) -> p h d", h=HEADS)
+                    .unsqueeze(1)
+                    .to_broadcast([P, BANK_ROWS, HEADS, HEAD_DIM]),
+                    op=ALU.add,
+                )
+
+            part = (g * GROUP) // TABLE_PART
+            rows = slice(g * GROUP - part * TABLE_PART, (g + 1) * GROUP - part * TABLE_PART)
+
+            def table(tile_, first_col, width):
+                return (
+                    tile_[:, rows, first_col : first_col + width]
+                    .unsqueeze(1)
+                    .to_broadcast([P, HEADS, GROUP, width])
+                )
+
+            low = slice(0, HALF)
+            high = slice(HALF, ROPE)
+            x_low = q_sb[:, :, :, NOPE : NOPE + HALF]
+            x_high = q_sb[:, :, :, NOPE + HALF : HEAD_DIM]
+            by_cos = rope_pool.tile([P, HEADS, GROUP, ROPE], F32, name="by_cos")
+            by_sin = rope_pool.tile([P, HEADS, GROUP, ROPE], F32, name="by_sin")
+            nc.vector.tensor_tensor(
+                out=by_cos[:],
+                in0=q_sb[:, :, :, NOPE:HEAD_DIM],
+                in1=table(cos_parts[part], 0, ROPE),
+                op=ALU.mult,
+            )
+            nc.vector.tensor_tensor(
+                out=by_sin[:, :, :, low], in0=x_high, in1=table(sin_parts[part], 0, HALF), op=ALU.mult
+            )
+            nc.vector.tensor_tensor(
+                out=by_sin[:, :, :, high], in0=x_low, in1=table(sin_parts[part], HALF, HALF), op=ALU.mult
+            )
+            nc.vector.tensor_tensor(
+                out=x_low, in0=by_cos[:, :, :, low], in1=by_sin[:, :, :, low], op=ALU.subtract
+            )
+            nc.vector.tensor_tensor(
+                out=x_high, in0=by_cos[:, :, :, high], in1=by_sin[:, :, :, high], op=ALU.add
+            )
+            nc.sync.dma_start(out=out_dram[:, :, g * GROUP : (g + 1) * GROUP, :], in_=q_sb[:])
+
+        packed = {}
+        for g in range(GROUPS + 1):
+            if g < GROUPS:
+                packed[g] = transpose_and_quantise(g)
+            if g >= 1:
+                project_and_rotate(g - 1, packed[g - 1][0], packed[g - 1][1])

@@ -11,6 +11,7 @@ U8 = mybir.dt.uint8
 FP8X4 = mybir.dt.float8_e4m3fn_x4
 FP4X4 = mybir.dt.float4_e2m1fn_x4
 ALU = mybir.AluOpType
+ACT = mybir.ActivationFunctionType
 
 P = 128
 PACK = 4
@@ -18,16 +19,18 @@ TOKENS = 8192
 HID = 512
 HEADS = 2
 HEAD_DIM = 128
-NOPE = 64
-ROPE = 64
-HALF = ROPE // 2
+SET = 64
+HALF = SET // 2
 FEATURES = HEADS * HEAD_DIM
+PLAIN = 0
+TURNED = 1
 ROWS = TOKENS // P
 GROUP = 4
 GROUPS = ROWS // GROUP
 BANK_ROWS = 2
 TABLE_PART = 16
 WORDS = HID // 2
+ONES = 32
 
 FLOPS = 2 * TOKENS * HID * FEATURES
 
@@ -45,52 +48,94 @@ def tile_gptossmlaattention_pb_t_kernel(
         const = pools.enter_context(tc.tile_pool(name="const", bufs=1))
         x_pool = pools.enter_context(tc.tile_pool(name="x", bufs=GROUPS))
         mx_pool = pools.enter_context(tc.tile_pool(name="mx", bufs=3))
-        rope_pool = pools.enter_context(tc.tile_pool(name="rope", bufs=2))
+        work = pools.enter_context(tc.tile_pool(name="work", bufs=3))
         out_pool = pools.enter_context(tc.tile_pool(name="outs", bufs=4))
-        words_psum = pools.enter_context(tc.psum_pool(name="words", bufs=4))
-        q_psum = pools.enter_context(tc.psum_pool(name="q", bufs=4))
+        flipped_psum = pools.enter_context(tc.psum_pool(name="flipped", bufs=2))
+        plain_psum = pools.enter_context(tc.psum_pool(name="plain", bufs=2))
+        turned_t_psum = pools.enter_context(tc.psum_pool(name="turned_t", bufs=2))
+        turned_psum = pools.enter_context(tc.psum_pool(name="turned", bufs=2))
 
-        ident = const.tile([P, P], F32)
-        make_identity(nc, ident[:])
-
-        w_scales = const.tile([P, FEATURES], U8, align_bytes=64)
-        nc.vector.memset(w_scales[:].bitcast(I32), 0)
-        w_words = const.tile([P, 2 * FEATURES], U8, align_bytes=64)
-        bias_bf = const.tile([P, FEATURES], BF16)
-        bias = const.tile([P, FEATURES], F32)
+        w_words = const.tile([P, 2, 2 * P], U8, align_bytes=64)
+        w_plane_in = const.tile([P, FEATURES], U8, align_bytes=64)
+        w_plane = const.tile([P, 2, P], U8, align_bytes=64)
+        bias_row = const.tile([P, 2, P], BF16)
+        nc.vector.memset(w_plane_in[:].bitcast(I32), 0)
+        nc.vector.memset(bias_row[:], 0.0)
 
         x_tiles = []
         cos_parts = []
         sin_parts = []
         for g in range(GROUPS):
-            rows = slice(g * GROUP, (g + 1) * GROUP)
             x_sb = x_pool.tile([P, GROUP, HID], BF16, name="x_sb")
-            nc.sync.dma_start(out=x_sb[:], in_=x_dram[:, rows, :])
+            nc.sync.dma_start(out=x_sb[:], in_=x_dram[:, g * GROUP : (g + 1) * GROUP, :])
             x_tiles.append(x_sb)
             if g == 0:
-                nc.sync.dma_start(out=w_words[:].bitcast(I32), in_=Wq_words[0].bitcast(I32))
+                words_by_set = Wq_words[0].bitcast(I32).rearrange(
+                    "p (h s b) -> p s h b", h=HEADS, s=2
+                )
+                bias_by_set = bq.rearrange("(o h s j) -> o s h j", o=1, h=HEADS, s=2)
+                for s in (PLAIN, TURNED):
+                    nc.sync.dma_start(
+                        out=w_words[:, s, :].bitcast(I32).rearrange("p (h b) -> p h b", h=HEADS),
+                        in_=words_by_set[:, s, :, :],
+                    )
                 for quad in range(4):
                     nc.sync.dma_start(
-                        out=w_scales[32 * quad : 32 * quad + 4, :].bitcast(I32),
+                        out=w_plane_in[32 * quad : 32 * quad + 4, :].bitcast(I32),
                         in_=Wq_scales[0, 4 * quad : 4 * quad + 4, :].bitcast(I32),
                     )
-                nc.sync.dma_start(out=bias_bf[:], in_=bq.partition_broadcast(P))
+                for s in (PLAIN, TURNED):
+                    nc.sync.dma_start(
+                        out=bias_row[0:1, s, :].rearrange("o (h j) -> o h j", h=HEADS),
+                        in_=bias_by_set[:, s, :, :],
+                    )
             if (g * GROUP) % TABLE_PART == 0:
                 part = slice(g * GROUP, g * GROUP + TABLE_PART)
-                cos_sb = const.tile([P, TABLE_PART, ROPE], BF16, name="cos%d" % len(cos_parts))
-                sin_sb = const.tile([P, TABLE_PART, ROPE], BF16, name="sin%d" % len(sin_parts))
+                cos_sb = const.tile([P, TABLE_PART, SET], BF16, name="cos%d" % len(cos_parts))
+                sin_sb = const.tile([P, TABLE_PART, SET], BF16, name="sin%d" % len(sin_parts))
                 nc.sync.dma_start(out=cos_sb[:], in_=cos_dram[:, part, :])
                 nc.sync.dma_start(out=sin_sb[:], in_=sin_dram[:, part, :])
                 cos_parts.append(cos_sb)
                 sin_parts.append(sin_sb)
-        nc.scalar.copy(out=bias[:], in_=bias_bf[:])
+
+        ident = const.tile([P, P], F32)
+        make_identity(nc, ident[:])
+        ones = const.tile([P, P], BF16)
+        nc.vector.memset(ones[:], 1.0)
+
+        nc.vector.tensor_copy(
+            out=w_plane[:].bitcast(I32).rearrange("p s (h b) -> p s h b", h=HEADS),
+            in_=w_plane_in[:].bitcast(I32).rearrange("p (h s b) -> p s h b", h=HEADS, s=2),
+        )
+
+        bias_ps = plain_psum.tile([P, GROUP, P], F32, name="plain_ps")
+        nc.tensor.matmul(
+            out=bias_ps[:, 0:2, :].rearrange("p s f -> p (s f)"),
+            lhsT=ones[:],
+            rhs=bias_row[:].rearrange("p s f -> p (s f)"),
+            start=True,
+            stop=True,
+        )
+        nc.tensor.matmul(
+            out=bias_ps[:, 2, 0:ONES],
+            lhsT=bias_row[:, TURNED, :],
+            rhs=ones[:, 0:ONES],
+            start=True,
+            stop=True,
+        )
+        plain_bias = const.tile([P, HEADS, SET], F32)
+        turned_bias = const.tile([P, 1], F32)
+        nc.scalar.copy(
+            out=plain_bias[:], in_=bias_ps[:, PLAIN, :].rearrange("p (h j) -> p h j", h=HEADS)
+        )
+        nc.scalar.copy(out=turned_bias[:], in_=bias_ps[:, 2, 0:1])
 
         def transpose_and_quantise(g):
             x_words = x_tiles[g][:].bitcast(F32)
             grouped = mx_pool.tile([P, GROUP, P, PACK], BF16, align_bytes=64, name="grouped")
             grouped_words = grouped[:].bitcast(F32)
             for first in range(0, GROUP, BANK_ROWS):
-                flipped = words_psum.tile([P, BANK_ROWS, 2, P], F32, name="flipped")
+                flipped = flipped_psum.tile([P, BANK_ROWS, 2, P], F32, name="flipped")
                 for a in range(BANK_ROWS):
                     for u in range(2):
                         nc.tensor.transpose(
@@ -109,30 +154,46 @@ def tile_gptossmlaattention_pb_t_kernel(
             )
             return codes, scales
 
-        def project_and_rotate(g, codes, scales):
-            q_sb = out_pool.tile([P, HEADS, GROUP, HEAD_DIM], F32, name="q_sb")
-            for first in range(0, GROUP, BANK_ROWS):
-                q_ps = q_psum.tile([P, BANK_ROWS, FEATURES], F32, name="q_ps")
-                for a in range(BANK_ROWS):
-                    tokens = slice((first + a) * P, (first + a + 1) * P)
-                    nc.tensor.matmul_mx(
-                        out=q_ps[:, a, :],
-                        lhsT=codes[:, tokens].bitcast(FP8X4),
-                        lhsT_scale=scales[:, tokens],
-                        rhs=w_words[:].bitcast(FP4X4),
-                        rhs_scale=w_scales[:],
-                        start=True,
-                        stop=True,
-                    )
-                nc.vector.tensor_tensor(
-                    out=q_sb[:, :, first : first + BANK_ROWS, :].rearrange("p h a d -> p a h d"),
-                    in0=q_ps[:].rearrange("p a (h d) -> p a h d", h=HEADS),
-                    in1=bias[:]
-                    .rearrange("p (h d) -> p h d", h=HEADS)
-                    .unsqueeze(1)
-                    .to_broadcast([P, BANK_ROWS, HEADS, HEAD_DIM]),
-                    op=ALU.add,
+        def project(codes, scales):
+            turned_t_ps = turned_t_psum.tile([P, GROUP * P], F32, name="turned_t_ps")
+            nc.tensor.matmul_mx(
+                out=turned_t_ps[:],
+                lhsT=w_words[:, TURNED, :].bitcast(FP4X4),
+                lhsT_scale=w_plane[:, TURNED, :],
+                rhs=codes[:].bitcast(FP8X4),
+                rhs_scale=scales[:],
+                start=True,
+                stop=True,
+            )
+            plain_ps = plain_psum.tile([P, GROUP, P], F32, name="plain_ps")
+            for a in range(GROUP):
+                nc.tensor.matmul_mx(
+                    out=plain_ps[:, a, :],
+                    lhsT=codes[:, a * P : (a + 1) * P].bitcast(FP8X4),
+                    lhsT_scale=scales[:, a * P : (a + 1) * P],
+                    rhs=w_words[:, PLAIN, :].bitcast(FP4X4),
+                    rhs_scale=w_plane[:, PLAIN, :],
+                    start=True,
+                    stop=True,
                 )
+            turned_t = work.tile([P, GROUP * P], F32, name="turned_t")
+            nc.scalar.activation(
+                out=turned_t[:], in_=turned_t_ps[:], func=ACT.Identity, bias=turned_bias[:], scale=1.0
+            )
+            return plain_ps, turned_t
+
+        def rotate_and_store(g, plain_ps, turned_t):
+            turned_ps = turned_psum.tile([P, GROUP, P], F32, name="turned_ps")
+            for a in range(GROUP):
+                nc.tensor.transpose(turned_ps[:, a, :], turned_t[:, a * P : (a + 1) * P], ident[:])
+
+            q_sb = out_pool.tile([P, HEADS, GROUP, HEAD_DIM], F32, name="q_sb")
+            nc.vector.tensor_tensor(
+                out=q_sb[:, :, :, 0:SET],
+                in0=plain_ps[:].rearrange("p a (h j) -> p h a j", h=HEADS),
+                in1=plain_bias[:].unsqueeze(2).to_broadcast([P, HEADS, GROUP, SET]),
+                op=ALU.add,
+            )
 
             part = (g * GROUP) // TABLE_PART
             rows = slice(g * GROUP - part * TABLE_PART, (g + 1) * GROUP - part * TABLE_PART)
@@ -144,35 +205,46 @@ def tile_gptossmlaattention_pb_t_kernel(
                     .to_broadcast([P, HEADS, GROUP, width])
                 )
 
+            x = turned_ps[:].rearrange("p a (h j) -> p h a j", h=HEADS)
             low = slice(0, HALF)
-            high = slice(HALF, ROPE)
-            x_low = q_sb[:, :, :, NOPE : NOPE + HALF]
-            x_high = q_sb[:, :, :, NOPE + HALF : HEAD_DIM]
-            by_cos = rope_pool.tile([P, HEADS, GROUP, ROPE], F32, name="by_cos")
-            by_sin = rope_pool.tile([P, HEADS, GROUP, ROPE], F32, name="by_sin")
+            high = slice(HALF, SET)
+            by_cos = work.tile([P, HEADS, GROUP, SET], F32, name="by_cos")
+            by_sin = work.tile([P, HEADS, GROUP, SET], F32, name="by_sin")
             nc.vector.tensor_tensor(
-                out=by_cos[:],
-                in0=q_sb[:, :, :, NOPE:HEAD_DIM],
-                in1=table(cos_parts[part], 0, ROPE),
+                out=by_cos[:], in0=x, in1=table(cos_parts[part], 0, SET), op=ALU.mult
+            )
+            nc.vector.tensor_tensor(
+                out=by_sin[:, :, :, low],
+                in0=x[:, :, :, high],
+                in1=table(sin_parts[part], 0, HALF),
                 op=ALU.mult,
             )
             nc.vector.tensor_tensor(
-                out=by_sin[:, :, :, low], in0=x_high, in1=table(sin_parts[part], 0, HALF), op=ALU.mult
+                out=by_sin[:, :, :, high],
+                in0=x[:, :, :, low],
+                in1=table(sin_parts[part], HALF, HALF),
+                op=ALU.mult,
             )
-            nc.vector.tensor_tensor(
-                out=by_sin[:, :, :, high], in0=x_low, in1=table(sin_parts[part], HALF, HALF), op=ALU.mult
+            nc.gpsimd.tensor_tensor(
+                out=q_sb[:, :, :, SET : SET + HALF],
+                in0=by_cos[:, :, :, low],
+                in1=by_sin[:, :, :, low],
+                op=ALU.subtract,
             )
-            nc.vector.tensor_tensor(
-                out=x_low, in0=by_cos[:, :, :, low], in1=by_sin[:, :, :, low], op=ALU.subtract
-            )
-            nc.vector.tensor_tensor(
-                out=x_high, in0=by_cos[:, :, :, high], in1=by_sin[:, :, :, high], op=ALU.add
+            nc.gpsimd.tensor_tensor(
+                out=q_sb[:, :, :, SET + HALF : HEAD_DIM],
+                in0=by_cos[:, :, :, high],
+                in1=by_sin[:, :, :, high],
+                op=ALU.add,
             )
             nc.sync.dma_start(out=out_dram[:, :, g * GROUP : (g + 1) * GROUP, :], in_=q_sb[:])
 
         packed = {}
-        for g in range(GROUPS + 1):
-            if g < GROUPS:
-                packed[g] = transpose_and_quantise(g)
-            if g >= 1:
-                project_and_rotate(g - 1, packed[g - 1][0], packed[g - 1][1])
+        projected = {}
+        for i in range(GROUPS + 2):
+            if i < GROUPS:
+                packed[i] = transpose_and_quantise(i)
+            if i >= 2:
+                rotate_and_store(i - 2, projected[i - 2][0], projected[i - 2][1])
+            if 1 <= i <= GROUPS:
+                projected[i - 1] = project(packed[i - 1][0], packed[i - 1][1])

@@ -49,18 +49,20 @@ def tile_gptossmlaattention_pb_t_kernel(
         x_pool = pools.enter_context(tc.tile_pool(name="x", bufs=GROUPS))
         mx_pool = pools.enter_context(tc.tile_pool(name="mx", bufs=3))
         work = pools.enter_context(tc.tile_pool(name="work", bufs=3))
+        products = pools.enter_context(tc.tile_pool(name="products", bufs=4))
         out_pool = pools.enter_context(tc.tile_pool(name="outs", bufs=4))
         flipped_psum = pools.enter_context(tc.psum_pool(name="flipped", bufs=2))
         plain_psum = pools.enter_context(tc.psum_pool(name="plain", bufs=2))
         turned_t_psum = pools.enter_context(tc.psum_pool(name="turned_t", bufs=2))
         turned_psum = pools.enter_context(tc.psum_pool(name="turned", bufs=2))
+        pools.enter_context(tc.manual_schedule())
 
-        w_words = const.tile([P, 2, 2 * P], U8, align_bytes=64)
-        w_plane_in = const.tile([P, FEATURES], U8, align_bytes=64)
-        w_plane = const.tile([P, 2, P], U8, align_bytes=64)
-        bias_row = const.tile([P, 2, P], BF16)
+        w_words_in = const.tile([P, 2 * FEATURES], U8)
+        w_plane_in = const.tile([P, FEATURES], U8)
+        bias_in = const.tile([P, FEATURES], BF16)
         nc.vector.memset(w_plane_in[:].bitcast(I32), 0)
-        nc.vector.memset(bias_row[:], 0.0)
+        nc.vector.memset(bias_in[:], 0.0)
+        nc.scalar.dma_start(out=bias_in[0:1, :], in_=bq.rearrange("(o f) -> o f", o=1))
 
         x_tiles = []
         cos_parts = []
@@ -69,28 +71,15 @@ def tile_gptossmlaattention_pb_t_kernel(
             x_sb = x_pool.tile([P, GROUP, HID], BF16, name="x_sb")
             nc.sync.dma_start(out=x_sb[:], in_=x_dram[:, g * GROUP : (g + 1) * GROUP, :])
             x_tiles.append(x_sb)
-            if g == 0:
-                words_by_set = Wq_words[0].bitcast(I32).rearrange(
-                    "p (h s b) -> p s h b", h=HEADS, s=2
-                )
-                bias_by_set = bq.rearrange("(o h s j) -> o s h j", o=1, h=HEADS, s=2)
-                for s in (PLAIN, TURNED):
-                    nc.sync.dma_start(
-                        out=w_words[:, s, :].bitcast(I32).rearrange("p (h b) -> p h b", h=HEADS),
-                        in_=words_by_set[:, s, :, :],
-                    )
+            if g == 1:
+                nc.sync.dma_start(out=w_words_in[:].bitcast(I32), in_=Wq_words[0].bitcast(I32))
                 for quad in range(4):
                     nc.sync.dma_start(
                         out=w_plane_in[32 * quad : 32 * quad + 4, :].bitcast(I32),
                         in_=Wq_scales[0, 4 * quad : 4 * quad + 4, :].bitcast(I32),
                     )
-                for s in (PLAIN, TURNED):
-                    nc.sync.dma_start(
-                        out=bias_row[0:1, s, :].rearrange("o (h j) -> o h j", h=HEADS),
-                        in_=bias_by_set[:, s, :, :],
-                    )
-            if (g * GROUP) % TABLE_PART == 0:
-                part = slice(g * GROUP, g * GROUP + TABLE_PART)
+            if (g * GROUP) % TABLE_PART == 2 * GROUP:
+                part = slice((g - 2) * GROUP, (g - 2) * GROUP + TABLE_PART)
                 cos_sb = const.tile([P, TABLE_PART, SET], BF16, name="cos%d" % len(cos_parts))
                 sin_sb = const.tile([P, TABLE_PART, SET], BF16, name="sin%d" % len(sin_parts))
                 nc.sync.dma_start(out=cos_sb[:], in_=cos_dram[:, part, :])
@@ -103,10 +92,18 @@ def tile_gptossmlaattention_pb_t_kernel(
         ones = const.tile([P, P], BF16)
         nc.vector.memset(ones[:], 1.0)
 
-        nc.vector.tensor_copy(
-            out=w_plane[:].bitcast(I32).rearrange("p s (h b) -> p s h b", h=HEADS),
-            in_=w_plane_in[:].bitcast(I32).rearrange("p (h s b) -> p s h b", h=HEADS, s=2),
-        )
+        w_words = const.tile([P, 2, 2 * P], U8, align_bytes=64)
+        w_plane = const.tile([P, 2, P], U8, align_bytes=64)
+        bias_row = const.tile([P, 2, P], BF16)
+        for sorted_, given in (
+            (bias_row[:], bias_in[:]),
+            (w_words[:].bitcast(I32), w_words_in[:].bitcast(I32)),
+            (w_plane[:].bitcast(I32), w_plane_in[:].bitcast(I32)),
+        ):
+            nc.vector.tensor_copy(
+                out=sorted_.rearrange("p s (h b) -> p s h b", h=HEADS),
+                in_=given.rearrange("p (h s b) -> p s h b", h=HEADS, s=2),
+            )
 
         bias_ps = plain_psum.tile([P, GROUP, P], F32, name="plain_ps")
         nc.tensor.matmul(
@@ -188,53 +185,43 @@ def tile_gptossmlaattention_pb_t_kernel(
                 nc.tensor.transpose(turned_ps[:, a, :], turned_t[:, a * P : (a + 1) * P], ident[:])
 
             q_sb = out_pool.tile([P, HEADS, GROUP, HEAD_DIM], F32, name="q_sb")
-            nc.vector.tensor_tensor(
-                out=q_sb[:, :, :, 0:SET],
-                in0=plain_ps[:].rearrange("p a (h j) -> p h a j", h=HEADS),
-                in1=plain_bias[:].unsqueeze(2).to_broadcast([P, HEADS, GROUP, SET]),
-                op=ALU.add,
-            )
 
             part = (g * GROUP) // TABLE_PART
             rows = slice(g * GROUP - part * TABLE_PART, (g + 1) * GROUP - part * TABLE_PART)
 
-            def table(tile_, first_col, width):
+            def table(tile_, first_col):
                 return (
-                    tile_[:, rows, first_col : first_col + width]
+                    tile_[:, rows, first_col : first_col + HALF]
                     .unsqueeze(1)
-                    .to_broadcast([P, HEADS, GROUP, width])
+                    .to_broadcast([P, HEADS, GROUP, HALF])
                 )
 
             x = turned_ps[:].rearrange("p a (h j) -> p h a j", h=HEADS)
-            low = slice(0, HALF)
-            high = slice(HALF, SET)
-            by_cos = work.tile([P, HEADS, GROUP, SET], F32, name="by_cos")
-            by_sin = work.tile([P, HEADS, GROUP, SET], F32, name="by_sin")
+            for first_col, other_col, join in ((0, HALF, ALU.subtract), (HALF, 0, ALU.add)):
+                by_cos = products.tile([P, HEADS, GROUP, HALF], F32, name="by_cos")
+                by_sin = products.tile([P, HEADS, GROUP, HALF], F32, name="by_sin")
+                nc.vector.tensor_tensor(
+                    out=by_cos[:],
+                    in0=x[:, :, :, first_col : first_col + HALF],
+                    in1=table(cos_parts[part], first_col),
+                    op=ALU.mult,
+                )
+                nc.vector.tensor_tensor(
+                    out=by_sin[:],
+                    in0=x[:, :, :, other_col : other_col + HALF],
+                    in1=table(sin_parts[part], first_col),
+                    op=ALU.mult,
+                )
+                nc.gpsimd.tensor_tensor(
+                    out=q_sb[:, :, :, SET + first_col : SET + first_col + HALF],
+                    in0=by_cos[:],
+                    in1=by_sin[:],
+                    op=join,
+                )
             nc.vector.tensor_tensor(
-                out=by_cos[:], in0=x, in1=table(cos_parts[part], 0, SET), op=ALU.mult
-            )
-            nc.vector.tensor_tensor(
-                out=by_sin[:, :, :, low],
-                in0=x[:, :, :, high],
-                in1=table(sin_parts[part], 0, HALF),
-                op=ALU.mult,
-            )
-            nc.vector.tensor_tensor(
-                out=by_sin[:, :, :, high],
-                in0=x[:, :, :, low],
-                in1=table(sin_parts[part], HALF, HALF),
-                op=ALU.mult,
-            )
-            nc.gpsimd.tensor_tensor(
-                out=q_sb[:, :, :, SET : SET + HALF],
-                in0=by_cos[:, :, :, low],
-                in1=by_sin[:, :, :, low],
-                op=ALU.subtract,
-            )
-            nc.gpsimd.tensor_tensor(
-                out=q_sb[:, :, :, SET + HALF : HEAD_DIM],
-                in0=by_cos[:, :, :, high],
-                in1=by_sin[:, :, :, high],
+                out=q_sb[:, :, :, 0:SET],
+                in0=plain_ps[:].rearrange("p a (h j) -> p h a j", h=HEADS),
+                in1=plain_bias[:].unsqueeze(2).to_broadcast([P, HEADS, GROUP, SET]),
                 op=ALU.add,
             )
             nc.sync.dma_start(out=out_dram[:, :, g * GROUP : (g + 1) * GROUP, :], in_=q_sb[:])

@@ -29,6 +29,9 @@ GROUP = 4
 GROUPS = ROWS // GROUP
 BANK_ROWS = 2
 TABLE_PART = 16
+PART_GROUPS = TABLE_PART // GROUP
+COS = 0
+SIN = 1
 WORDS = HID // 2
 ONES = 32
 
@@ -49,8 +52,8 @@ def tile_gptossmlaattention_pb_t_kernel(
         x_pool = pools.enter_context(tc.tile_pool(name="x", bufs=GROUPS))
         mx_pool = pools.enter_context(tc.tile_pool(name="mx", bufs=3))
         work = pools.enter_context(tc.tile_pool(name="work", bufs=3))
-        products = pools.enter_context(tc.tile_pool(name="products", bufs=4))
-        out_pool = pools.enter_context(tc.tile_pool(name="outs", bufs=4))
+        products = pools.enter_context(tc.tile_pool(name="products", bufs=3))
+        out_pool = pools.enter_context(tc.tile_pool(name="outs", bufs=GROUPS))
         flipped_psum = pools.enter_context(tc.psum_pool(name="flipped", bufs=2))
         plain_psum = pools.enter_context(tc.psum_pool(name="plain", bufs=2))
         turned_t_psum = pools.enter_context(tc.psum_pool(name="turned_t", bufs=2))
@@ -65,7 +68,7 @@ def tile_gptossmlaattention_pb_t_kernel(
         nc.scalar.dma_start(out=bias_in[0:1, :], in_=bq.rearrange("(o f) -> o f", o=1))
 
         x_tiles = []
-        cos_parts = []
+        table_parts = []
         sin_parts = []
         for g in range(GROUPS):
             x_sb = x_pool.tile([P, GROUP, HID], BF16, name="x_sb")
@@ -80,11 +83,16 @@ def tile_gptossmlaattention_pb_t_kernel(
                     )
             if (g * GROUP) % TABLE_PART == 2 * GROUP:
                 part = slice((g - 2) * GROUP, (g - 2) * GROUP + TABLE_PART)
-                cos_sb = const.tile([P, TABLE_PART, SET], BF16, name="cos%d" % len(cos_parts))
+                tables = const.tile(
+                    [P, PART_GROUPS, 2, GROUP, SET], BF16, name="tables%d" % len(table_parts)
+                )
                 sin_sb = const.tile([P, TABLE_PART, SET], BF16, name="sin%d" % len(sin_parts))
-                nc.sync.dma_start(out=cos_sb[:], in_=cos_dram[:, part, :])
+                nc.sync.dma_start(
+                    out=tables[:, :, COS, :, :],
+                    in_=cos_dram[:, part, :].rearrange("p (g a) j -> p g a j", a=GROUP),
+                )
                 nc.sync.dma_start(out=sin_sb[:], in_=sin_dram[:, part, :])
-                cos_parts.append(cos_sb)
+                table_parts.append(tables)
                 sin_parts.append(sin_sb)
 
         ident = const.tile([P, P], F32)
@@ -126,6 +134,15 @@ def tile_gptossmlaattention_pb_t_kernel(
             out=plain_bias[:], in_=bias_ps[:, PLAIN, :].rearrange("p (h j) -> p h j", h=HEADS)
         )
         nc.scalar.copy(out=turned_bias[:], in_=bias_ps[:, 2, 0:1])
+
+        def swap_sin(part):
+            for mine, other in ((0, HALF), (HALF, 0)):
+                nc.scalar.copy(
+                    out=table_parts[part][:, :, SIN, :, mine : mine + HALF],
+                    in_=sin_parts[part][:, :, other : other + HALF].rearrange(
+                        "p (g a) j -> p g a j", a=GROUP
+                    ),
+                )
 
         def transpose_and_quantise(g):
             x_words = x_tiles[g][:].bitcast(F32)
@@ -185,45 +202,32 @@ def tile_gptossmlaattention_pb_t_kernel(
                 nc.tensor.transpose(turned_ps[:, a, :], turned_t[:, a * P : (a + 1) * P], ident[:])
 
             q_sb = out_pool.tile([P, HEADS, GROUP, HEAD_DIM], F32, name="q_sb")
-
-            part = (g * GROUP) // TABLE_PART
-            rows = slice(g * GROUP - part * TABLE_PART, (g + 1) * GROUP - part * TABLE_PART)
-
-            def table(tile_, first_col):
-                return (
-                    tile_[:, rows, first_col : first_col + HALF]
-                    .unsqueeze(1)
-                    .to_broadcast([P, HEADS, GROUP, HALF])
-                )
-
-            x = turned_ps[:].rearrange("p a (h j) -> p h a j", h=HEADS)
-            for first_col, other_col, join in ((0, HALF, ALU.subtract), (HALF, 0, ALU.add)):
-                by_cos = products.tile([P, HEADS, GROUP, HALF], F32, name="by_cos")
-                by_sin = products.tile([P, HEADS, GROUP, HALF], F32, name="by_sin")
-                nc.vector.tensor_tensor(
-                    out=by_cos[:],
-                    in0=x[:, :, :, first_col : first_col + HALF],
-                    in1=table(cos_parts[part], first_col),
-                    op=ALU.mult,
-                )
-                nc.vector.tensor_tensor(
-                    out=by_sin[:],
-                    in0=x[:, :, :, other_col : other_col + HALF],
-                    in1=table(sin_parts[part], first_col),
-                    op=ALU.mult,
-                )
-                nc.gpsimd.tensor_tensor(
-                    out=q_sb[:, :, :, SET + first_col : SET + first_col + HALF],
-                    in0=by_cos[:],
-                    in1=by_sin[:],
-                    op=join,
-                )
             nc.vector.tensor_tensor(
                 out=q_sb[:, :, :, 0:SET],
                 in0=plain_ps[:].rearrange("p a (h j) -> p h a j", h=HEADS),
                 in1=plain_bias[:].unsqueeze(2).to_broadcast([P, HEADS, GROUP, SET]),
                 op=ALU.add,
             )
+            shape = [P, 2, GROUP, HEADS, SET]
+            by_table = products.tile(shape, F32, name="by_table")
+            nc.vector.tensor_tensor(
+                out=by_table[:],
+                in0=turned_ps[:]
+                .rearrange("p a (h j) -> p a h j", h=HEADS)
+                .unsqueeze(1)
+                .to_broadcast(shape),
+                in1=table_parts[g // PART_GROUPS][:, g % PART_GROUPS, :, :, :]
+                .unsqueeze(3)
+                .to_broadcast(shape),
+                op=ALU.mult,
+            )
+            for mine, other, join in ((0, HALF, ALU.subtract), (HALF, 0, ALU.add)):
+                nc.gpsimd.tensor_tensor(
+                    out=q_sb[:, :, :, SET + mine : SET + mine + HALF],
+                    in0=by_table[:, COS, :, :, mine : mine + HALF].rearrange("p a h j -> p h a j"),
+                    in1=by_table[:, SIN, :, :, other : other + HALF].rearrange("p a h j -> p h a j"),
+                    op=join,
+                )
             nc.sync.dma_start(out=out_dram[:, :, g * GROUP : (g + 1) * GROUP, :], in_=q_sb[:])
 
         packed = {}
@@ -235,3 +239,5 @@ def tile_gptossmlaattention_pb_t_kernel(
                 rotate_and_store(i - 2, projected[i - 2][0], projected[i - 2][1])
             if 1 <= i <= GROUPS:
                 projected[i - 1] = project(packed[i - 1][0], packed[i - 1][1])
+                if (i - 1) % PART_GROUPS == 0:
+                    swap_sin((i - 1) // PART_GROUPS)

@@ -52,7 +52,6 @@ def tile_gptossmlaattention_pb_t_kernel(
         x_pool = pools.enter_context(tc.tile_pool(name="x", bufs=GROUPS))
         mx_pool = pools.enter_context(tc.tile_pool(name="mx", bufs=3))
         work = pools.enter_context(tc.tile_pool(name="work", bufs=3))
-        products = pools.enter_context(tc.tile_pool(name="products", bufs=3))
         out_pool = pools.enter_context(tc.tile_pool(name="outs", bufs=GROUPS))
         flipped_psum = pools.enter_context(tc.psum_pool(name="flipped", bufs=2))
         plain_psum = pools.enter_context(tc.psum_pool(name="plain", bufs=2))
@@ -87,11 +86,11 @@ def tile_gptossmlaattention_pb_t_kernel(
                     [P, PART_GROUPS, 2, GROUP, SET], BF16, name="tables%d" % len(table_parts)
                 )
                 sin_sb = const.tile([P, TABLE_PART, SET], BF16, name="sin%d" % len(sin_parts))
+                nc.sync.dma_start(out=sin_sb[:], in_=sin_dram[:, part, :])
                 nc.sync.dma_start(
                     out=tables[:, :, COS, :, :],
                     in_=cos_dram[:, part, :].rearrange("p (g a) j -> p g a j", a=GROUP),
                 )
-                nc.sync.dma_start(out=sin_sb[:], in_=sin_dram[:, part, :])
                 table_parts.append(tables)
                 sin_parts.append(sin_sb)
 
@@ -99,41 +98,41 @@ def tile_gptossmlaattention_pb_t_kernel(
         make_identity(nc, ident[:])
         ones = const.tile([P, P], BF16)
         nc.vector.memset(ones[:], 1.0)
-
         w_words = const.tile([P, 2, 2 * P], U8, align_bytes=64)
         w_plane = const.tile([P, 2, P], U8, align_bytes=64)
         bias_row = const.tile([P, 2, P], BF16)
-        for sorted_, given in (
-            (bias_row[:], bias_in[:]),
-            (w_words[:].bitcast(I32), w_words_in[:].bitcast(I32)),
-            (w_plane[:].bitcast(I32), w_plane_in[:].bitcast(I32)),
-        ):
-            nc.vector.tensor_copy(
-                out=sorted_.rearrange("p s (h b) -> p s h b", h=HEADS),
-                in_=given.rearrange("p (h s b) -> p s h b", h=HEADS, s=2),
-            )
-
-        bias_ps = plain_psum.tile([P, GROUP, P], F32, name="plain_ps")
-        nc.tensor.matmul(
-            out=bias_ps[:, 0:2, :].rearrange("p s f -> p (s f)"),
-            lhsT=ones[:],
-            rhs=bias_row[:].rearrange("p s f -> p (s f)"),
-            start=True,
-            stop=True,
-        )
-        nc.tensor.matmul(
-            out=bias_ps[:, 2, 0:ONES],
-            lhsT=bias_row[:, TURNED, :],
-            rhs=ones[:, 0:ONES],
-            start=True,
-            stop=True,
-        )
         plain_bias = const.tile([P, HEADS, SET], F32)
         turned_bias = const.tile([P, 1], F32)
-        nc.scalar.copy(
-            out=plain_bias[:], in_=bias_ps[:, PLAIN, :].rearrange("p (h j) -> p h j", h=HEADS)
-        )
-        nc.scalar.copy(out=turned_bias[:], in_=bias_ps[:, 2, 0:1])
+
+        def sort_weight_and_bias():
+            for sorted_, given in (
+                (bias_row[:], bias_in[:]),
+                (w_words[:].bitcast(I32), w_words_in[:].bitcast(I32)),
+                (w_plane[:].bitcast(I32), w_plane_in[:].bitcast(I32)),
+            ):
+                nc.vector.tensor_copy(
+                    out=sorted_.rearrange("p s (h b) -> p s h b", h=HEADS),
+                    in_=given.rearrange("p (h s b) -> p s h b", h=HEADS, s=2),
+                )
+            bias_ps = plain_psum.tile([P, GROUP, P], F32, name="plain_ps")
+            nc.tensor.matmul(
+                out=bias_ps[:, 0:2, :].rearrange("p s f -> p (s f)"),
+                lhsT=ones[:],
+                rhs=bias_row[:].rearrange("p s f -> p (s f)"),
+                start=True,
+                stop=True,
+            )
+            nc.tensor.matmul(
+                out=bias_ps[:, 2, 0:ONES],
+                lhsT=bias_row[:, TURNED, :],
+                rhs=ones[:, 0:ONES],
+                start=True,
+                stop=True,
+            )
+            nc.scalar.copy(
+                out=plain_bias[:], in_=bias_ps[:, PLAIN, :].rearrange("p (h j) -> p h j", h=HEADS)
+            )
+            nc.scalar.copy(out=turned_bias[:], in_=bias_ps[:, 2, 0:1])
 
         def swap_sin(part):
             for mine, other in ((0, HALF), (HALF, 0)):
@@ -144,7 +143,7 @@ def tile_gptossmlaattention_pb_t_kernel(
                     ),
                 )
 
-        def transpose_and_quantise(g):
+        def flip(g):
             x_words = x_tiles[g][:].bitcast(F32)
             grouped = mx_pool.tile([P, GROUP, P, PACK], BF16, align_bytes=64, name="grouped")
             grouped_words = grouped[:].bitcast(F32)
@@ -159,6 +158,9 @@ def tile_gptossmlaattention_pb_t_kernel(
                     out=grouped_words[:, first : first + BANK_ROWS, :, :],
                     in_=flipped[:].rearrange("p a u r -> p a r u"),
                 )
+            return grouped
+
+        def quantise(grouped):
             codes = mx_pool.tile([P, GROUP * P], U32, align_bytes=64, name="codes")
             scales = mx_pool.tile([P, GROUP * P], U8, align_bytes=64, name="scales")
             nc.vector.quantize_mx(
@@ -196,11 +198,13 @@ def tile_gptossmlaattention_pb_t_kernel(
             )
             return plain_ps, turned_t
 
-        def rotate_and_store(g, plain_ps, turned_t):
+        def flip_back(turned_t):
             turned_ps = turned_psum.tile([P, GROUP, P], F32, name="turned_ps")
             for a in range(GROUP):
                 nc.tensor.transpose(turned_ps[:, a, :], turned_t[:, a * P : (a + 1) * P], ident[:])
+            return turned_ps
 
+        def add_plain_bias(plain_ps):
             q_sb = out_pool.tile([P, HEADS, GROUP, HEAD_DIM], F32, name="q_sb")
             nc.vector.tensor_tensor(
                 out=q_sb[:, :, :, 0:SET],
@@ -208,8 +212,11 @@ def tile_gptossmlaattention_pb_t_kernel(
                 in1=plain_bias[:].unsqueeze(2).to_broadcast([P, HEADS, GROUP, SET]),
                 op=ALU.add,
             )
+            return q_sb
+
+        def rotate_and_store(g, turned_ps, q_sb):
             shape = [P, 2, GROUP, HEADS, SET]
-            by_table = products.tile(shape, F32, name="by_table")
+            by_table = work.tile(shape, F32, name="by_table")
             nc.vector.tensor_tensor(
                 out=by_table[:],
                 in0=turned_ps[:]
@@ -230,14 +237,22 @@ def tile_gptossmlaattention_pb_t_kernel(
                 )
             nc.sync.dma_start(out=out_dram[:, :, g * GROUP : (g + 1) * GROUP, :], in_=q_sb[:])
 
-        packed = {}
-        projected = {}
-        for i in range(GROUPS + 2):
+        packed = {0: quantise(flip(0))}
+        sort_weight_and_bias()
+        turned_ts = {}
+        results = {}
+        for i in range(1, GROUPS + 2):
             if i < GROUPS:
-                packed[i] = transpose_and_quantise(i)
+                grouped = flip(i)
             if i >= 2:
-                rotate_and_store(i - 2, projected[i - 2][0], projected[i - 2][1])
-            if 1 <= i <= GROUPS:
-                projected[i - 1] = project(packed[i - 1][0], packed[i - 1][1])
+                turned_ps = flip_back(turned_ts[i - 2])
+            if i <= GROUPS:
+                plain_ps, turned_ts[i - 1] = project(packed[i - 1][0], packed[i - 1][1])
                 if (i - 1) % PART_GROUPS == 0:
                     swap_sin((i - 1) // PART_GROUPS)
+            if i < GROUPS:
+                packed[i] = quantise(grouped)
+            if i <= GROUPS:
+                results[i - 1] = add_plain_bias(plain_ps)
+            if i >= 2:
+                rotate_and_store(i - 2, turned_ps, results[i - 2])

@@ -206,15 +206,18 @@ def tile_gptossmlaattention_pb_t_kernel(
 
         def add_plain_bias(plain_ps):
             q_sb = out_pool.tile([P, HEADS, GROUP, HEAD_DIM], F32, name="q_sb")
+            fill_plain(plain_ps, q_sb)
+            return q_sb
+
+        def fill_plain(plain_ps, q_sb):
             nc.vector.tensor_tensor(
                 out=q_sb[:, :, :, 0:SET],
                 in0=plain_ps[:].rearrange("p a (h j) -> p h a j", h=HEADS),
                 in1=plain_bias[:].unsqueeze(2).to_broadcast([P, HEADS, GROUP, SET]),
                 op=ALU.add,
             )
-            return q_sb
 
-        def rotate_and_store(g, turned_ps, q_sb):
+        def multiply_tables(g, turned_ps):
             shape = [P, 2, GROUP, HEADS, SET]
             by_table = work.tile(shape, F32, name="by_table")
             nc.vector.tensor_tensor(
@@ -228,31 +231,46 @@ def tile_gptossmlaattention_pb_t_kernel(
                 .to_broadcast(shape),
                 op=ALU.mult,
             )
-            for mine, other, join in ((0, HALF, ALU.subtract), (HALF, 0, ALU.add)):
-                nc.gpsimd.tensor_tensor(
-                    out=q_sb[:, :, :, SET + mine : SET + mine + HALF],
-                    in0=by_table[:, COS, :, :, mine : mine + HALF].rearrange("p a h j -> p h a j"),
-                    in1=by_table[:, SIN, :, :, other : other + HALF].rearrange("p a h j -> p h a j"),
-                    op=join,
-                )
+            return by_table
+
+        def join(engine, by_table, q_sb, mine, other, op):
+            engine.tensor_tensor(
+                out=q_sb[:, :, :, SET + mine : SET + mine + HALF],
+                in0=by_table[:, COS, :, :, mine : mine + HALF].rearrange("p a h j -> p h a j"),
+                in1=by_table[:, SIN, :, :, other : other + HALF].rearrange("p a h j -> p h a j"),
+                op=op,
+            )
+
+        def store(g, q_sb):
             nc.sync.dma_start(out=out_dram[:, :, g * GROUP : (g + 1) * GROUP, :], in_=q_sb[:])
+
+        def rotate_and_store(g, turned_ps, q_sb):
+            by_table = multiply_tables(g, turned_ps)
+            join(nc.gpsimd, by_table, q_sb, 0, HALF, ALU.subtract)
+            join(nc.gpsimd, by_table, q_sb, HALF, 0, ALU.add)
+            store(g, q_sb)
 
         packed = {0: quantise(flip(0))}
         sort_weight_and_bias()
         turned_ts = {}
         results = {}
-        for i in range(1, GROUPS + 2):
+        for i in range(1, GROUPS + 1):
             if i < GROUPS:
                 grouped = flip(i)
             if i >= 2:
                 turned_ps = flip_back(turned_ts[i - 2])
-            if i <= GROUPS:
-                plain_ps, turned_ts[i - 1] = project(packed[i - 1][0], packed[i - 1][1])
-                if (i - 1) % PART_GROUPS == 0:
-                    swap_sin((i - 1) // PART_GROUPS)
+            plain_ps, turned_ts[i - 1] = project(packed[i - 1][0], packed[i - 1][1])
+            if (i - 1) % PART_GROUPS == 0:
+                swap_sin((i - 1) // PART_GROUPS)
             if i < GROUPS:
                 packed[i] = quantise(grouped)
-            if i <= GROUPS:
                 results[i - 1] = add_plain_bias(plain_ps)
             if i >= 2:
                 rotate_and_store(i - 2, turned_ps, results[i - 2])
+        last = GROUPS - 1
+        q_sb = out_pool.tile([P, HEADS, GROUP, HEAD_DIM], F32, name="q_sb")
+        by_table = multiply_tables(last, flip_back(turned_ts[last]))
+        join(nc.gpsimd, by_table, q_sb, 0, HALF, ALU.subtract)
+        fill_plain(plain_ps, q_sb)
+        join(nc.vector, by_table, q_sb, HALF, 0, ALU.add)
+        store(last, q_sb)

@@ -104,16 +104,17 @@ def tile_gptossmlaattention_pb_t_kernel(
         plain_bias = const.tile([P, HEADS, SET], F32)
         turned_bias = const.tile([P, 1], F32)
 
-        def sort_weight_and_bias():
-            for sorted_, given in (
-                (bias_row[:], bias_in[:]),
-                (w_words[:].bitcast(I32), w_words_in[:].bitcast(I32)),
-                (w_plane[:].bitcast(I32), w_plane_in[:].bitcast(I32)),
-            ):
-                nc.vector.tensor_copy(
-                    out=sorted_.rearrange("p s (h b) -> p s h b", h=HEADS),
-                    in_=given.rearrange("p (h s b) -> p s h b", h=HEADS, s=2),
-                )
+        def sort_by_set(sorted_, given):
+            nc.vector.tensor_copy(
+                out=sorted_.rearrange("p s (h b) -> p s h b", h=HEADS),
+                in_=given.rearrange("p (h s b) -> p s h b", h=HEADS, s=2),
+            )
+
+        def sort_weight():
+            sort_by_set(w_words[:].bitcast(I32), w_words_in[:].bitcast(I32))
+            sort_by_set(w_plane[:].bitcast(I32), w_plane_in[:].bitcast(I32))
+
+        def spread_bias():
             bias_ps = plain_psum.tile([P, GROUP, P], F32, name="plain_ps")
             nc.tensor.matmul(
                 out=bias_ps[:, 0:2, :].rearrange("p s f -> p (s f)"),
@@ -134,9 +135,9 @@ def tile_gptossmlaattention_pb_t_kernel(
             )
             nc.scalar.copy(out=turned_bias[:], in_=bias_ps[:, 2, 0:1])
 
-        def swap_sin(part):
+        def swap_sin(part, copy):
             for mine, other in ((0, HALF), (HALF, 0)):
-                nc.scalar.copy(
+                copy(
                     out=table_parts[part][:, :, SIN, :, mine : mine + HALF],
                     in_=sin_parts[part][:, :, other : other + HALF].rearrange(
                         "p (g a) j -> p g a j", a=GROUP
@@ -250,8 +251,11 @@ def tile_gptossmlaattention_pb_t_kernel(
             join(nc.gpsimd, by_table, q_sb, HALF, 0, ALU.add)
             store(g, q_sb)
 
-        packed = {0: quantise(flip(0))}
-        sort_weight_and_bias()
+        sort_by_set(bias_row[:], bias_in[:])
+        grouped = flip(0)
+        spread_bias()
+        packed = {0: quantise(grouped)}
+        sort_weight()
         turned_ts = {}
         results = {}
         for i in range(1, GROUPS + 1):
@@ -260,11 +264,13 @@ def tile_gptossmlaattention_pb_t_kernel(
             if i >= 2:
                 turned_ps = flip_back(turned_ts[i - 2])
             plain_ps, turned_ts[i - 1] = project(packed[i - 1][0], packed[i - 1][1])
-            if (i - 1) % PART_GROUPS == 0:
-                swap_sin((i - 1) // PART_GROUPS)
+            if (i - 1) % PART_GROUPS == 0 and i > 1:
+                swap_sin((i - 1) // PART_GROUPS, nc.scalar.copy)
             if i < GROUPS:
                 packed[i] = quantise(grouped)
                 results[i - 1] = add_plain_bias(plain_ps)
+            if i == 1:
+                swap_sin(0, nc.vector.tensor_copy)
             if i >= 2:
                 rotate_and_store(i - 2, turned_ps, results[i - 2])
         last = GROUPS - 1

@@ -34,6 +34,8 @@ COS = 0
 SIN = 1
 WORDS = HID // 2
 ONES = 32
+LOADED_ALONE = 4
+STORED_ALONE = 4
 
 FLOPS = 2 * TOKENS * HID * FEATURES
 
@@ -49,10 +51,8 @@ def tile_gptossmlaattention_pb_t_kernel(
 
     with ExitStack() as pools:
         const = pools.enter_context(tc.tile_pool(name="const", bufs=1))
-        x_pool = pools.enter_context(tc.tile_pool(name="x", bufs=GROUPS))
         mx_pool = pools.enter_context(tc.tile_pool(name="mx", bufs=3))
         work = pools.enter_context(tc.tile_pool(name="work", bufs=3))
-        out_pool = pools.enter_context(tc.tile_pool(name="outs", bufs=GROUPS))
         flipped_psum = pools.enter_context(tc.psum_pool(name="flipped", bufs=2))
         plain_psum = pools.enter_context(tc.psum_pool(name="plain", bufs=2))
         turned_t_psum = pools.enter_context(tc.psum_pool(name="turned_t", bufs=2))
@@ -70,9 +70,14 @@ def tile_gptossmlaattention_pb_t_kernel(
         table_parts = []
         sin_parts = []
         for g in range(GROUPS):
-            x_sb = x_pool.tile([P, GROUP, HID], BF16, name="x_sb")
-            nc.sync.dma_start(out=x_sb[:], in_=x_dram[:, g * GROUP : (g + 1) * GROUP, :])
-            x_tiles.append(x_sb)
+            together = 1 if g < LOADED_ALONE else 2
+            if g % together == 0:
+                x_sb = const.tile([P, together * GROUP, HID], BF16, name="x%d" % g)
+                nc.sync.dma_start(
+                    out=x_sb[:], in_=x_dram[:, g * GROUP : (g + together) * GROUP, :]
+                )
+                for c in range(together):
+                    x_tiles.append(x_sb[:, c * GROUP : (c + 1) * GROUP, :])
             if g == 1:
                 nc.sync.dma_start(out=w_words_in[:].bitcast(I32), in_=Wq_words[0].bitcast(I32))
                 for quad in range(4):
@@ -93,6 +98,16 @@ def tile_gptossmlaattention_pb_t_kernel(
                 )
                 table_parts.append(tables)
                 sin_parts.append(sin_sb)
+
+        results = []
+        stores = {}
+        for g in range(GROUPS):
+            together = 2 if g < GROUPS - STORED_ALONE else 1
+            if g % together == 0:
+                q_tile = const.tile([P, HEADS, together * GROUP, HEAD_DIM], F32, name="q%d" % g)
+                for c in range(together):
+                    results.append(q_tile[:, :, c * GROUP : (c + 1) * GROUP, :])
+                stores[g + together - 1] = (g, q_tile)
 
         ident = const.tile([P, P], F32)
         make_identity(nc, ident[:])
@@ -145,7 +160,7 @@ def tile_gptossmlaattention_pb_t_kernel(
                 )
 
         def flip(g):
-            x_words = x_tiles[g][:].bitcast(F32)
+            x_words = x_tiles[g].bitcast(F32)
             grouped = mx_pool.tile([P, GROUP, P, PACK], BF16, align_bytes=64, name="grouped")
             grouped_words = grouped[:].bitcast(F32)
             for first in range(0, GROUP, BANK_ROWS):
@@ -205,11 +220,6 @@ def tile_gptossmlaattention_pb_t_kernel(
                 nc.tensor.transpose(turned_ps[:, a, :], turned_t[:, a * P : (a + 1) * P], ident[:])
             return turned_ps
 
-        def add_plain_bias(plain_ps):
-            q_sb = out_pool.tile([P, HEADS, GROUP, HEAD_DIM], F32, name="q_sb")
-            fill_plain(plain_ps, q_sb)
-            return q_sb
-
         def fill_plain(plain_ps, q_sb):
             nc.vector.tensor_tensor(
                 out=q_sb[:, :, :, 0:SET],
@@ -242,14 +252,18 @@ def tile_gptossmlaattention_pb_t_kernel(
                 op=op,
             )
 
-        def store(g, q_sb):
-            nc.sync.dma_start(out=out_dram[:, :, g * GROUP : (g + 1) * GROUP, :], in_=q_sb[:])
+        def store(g):
+            if g in stores:
+                first, q_tile = stores[g]
+                nc.sync.dma_start(
+                    out=out_dram[:, :, first * GROUP : (g + 1) * GROUP, :], in_=q_tile[:]
+                )
 
         def rotate_and_store(g, turned_ps, q_sb):
             by_table = multiply_tables(g, turned_ps)
             join(nc.gpsimd, by_table, q_sb, 0, HALF, ALU.subtract)
             join(nc.gpsimd, by_table, q_sb, HALF, 0, ALU.add)
-            store(g, q_sb)
+            store(g)
 
         sort_by_set(bias_row[:], bias_in[:])
         grouped = flip(0)
@@ -257,7 +271,6 @@ def tile_gptossmlaattention_pb_t_kernel(
         packed = {0: quantise(grouped)}
         sort_weight()
         turned_ts = {}
-        results = {}
         for i in range(1, GROUPS + 1):
             if i < GROUPS:
                 grouped = flip(i)
@@ -268,15 +281,14 @@ def tile_gptossmlaattention_pb_t_kernel(
                 swap_sin((i - 1) // PART_GROUPS, nc.scalar.copy)
             if i < GROUPS:
                 packed[i] = quantise(grouped)
-                results[i - 1] = add_plain_bias(plain_ps)
+                fill_plain(plain_ps, results[i - 1])
             if i == 1:
                 swap_sin(0, nc.vector.tensor_copy)
             if i >= 2:
                 rotate_and_store(i - 2, turned_ps, results[i - 2])
         last = GROUPS - 1
-        q_sb = out_pool.tile([P, HEADS, GROUP, HEAD_DIM], F32, name="q_sb")
         by_table = multiply_tables(last, flip_back(turned_ts[last]))
-        join(nc.gpsimd, by_table, q_sb, 0, HALF, ALU.subtract)
-        fill_plain(plain_ps, q_sb)
-        join(nc.vector, by_table, q_sb, HALF, 0, ALU.add)
-        store(last, q_sb)
+        join(nc.gpsimd, by_table, results[last], 0, HALF, ALU.subtract)
+        fill_plain(plain_ps, results[last])
+        join(nc.vector, by_table, results[last], HALF, 0, ALU.add)
+        store(last)

@@ -67,7 +67,7 @@ def tile_gptossmlaattention_pb_t_kernel(
         nc.scalar.dma_start(out=bias_in[0:1, :], in_=bq.rearrange("(o f) -> o f", o=1))
 
         x_tiles = []
-        table_parts = []
+        cos_parts = []
         sin_parts = []
         for g in range(GROUPS):
             together = 1 if g < LOADED_ALONE else 2
@@ -87,17 +87,12 @@ def tile_gptossmlaattention_pb_t_kernel(
                     )
             if (g * GROUP) % TABLE_PART == 2 * GROUP:
                 part = slice((g - 2) * GROUP, (g - 2) * GROUP + TABLE_PART)
-                tables = const.tile(
-                    [P, PART_GROUPS, 2, GROUP, SET], BF16, name="tables%d" % len(table_parts)
-                )
                 sin_sb = const.tile([P, TABLE_PART, SET], BF16, name="sin%d" % len(sin_parts))
+                cos_sb = const.tile([P, TABLE_PART, SET], BF16, name="cos%d" % len(cos_parts))
                 nc.sync.dma_start(out=sin_sb[:], in_=sin_dram[:, part, :])
-                nc.sync.dma_start(
-                    out=tables[:, :, COS, :, :],
-                    in_=cos_dram[:, part, :].rearrange("p (g a) j -> p g a j", a=GROUP),
-                )
-                table_parts.append(tables)
+                nc.sync.dma_start(out=cos_sb[:], in_=cos_dram[:, part, :])
                 sin_parts.append(sin_sb)
+                cos_parts.append(cos_sb)
 
         results = []
         stores = {}
@@ -150,14 +145,8 @@ def tile_gptossmlaattention_pb_t_kernel(
             )
             nc.scalar.copy(out=turned_bias[:], in_=bias_ps[:, 2, 0:1])
 
-        def swap_sin(part, copy):
-            for mine, other in ((0, HALF), (HALF, 0)):
-                copy(
-                    out=table_parts[part][:, :, SIN, :, mine : mine + HALF],
-                    in_=sin_parts[part][:, :, other : other + HALF].rearrange(
-                        "p (g a) j -> p g a j", a=GROUP
-                    ),
-                )
+        def sin_low(part):
+            return sin_parts[part][:, :, 0:HALF]
 
         def flip(g):
             x_words = x_tiles[g].bitcast(F32)
@@ -229,27 +218,28 @@ def tile_gptossmlaattention_pb_t_kernel(
             )
 
         def multiply_tables(g, turned_ps):
-            shape = [P, 2, GROUP, HEADS, SET]
-            by_table = work.tile(shape, F32, name="by_table")
-            nc.vector.tensor_tensor(
-                out=by_table[:],
-                in0=turned_ps[:]
-                .rearrange("p a (h j) -> p a h j", h=HEADS)
-                .unsqueeze(1)
-                .to_broadcast(shape),
-                in1=table_parts[g // PART_GROUPS][:, g % PART_GROUPS, :, :, :]
-                .unsqueeze(3)
-                .to_broadcast(shape),
-                op=ALU.mult,
-            )
+            shape = [P, GROUP, HEADS, 2, HALF]
+            rows = slice((g % PART_GROUPS) * GROUP, (g % PART_GROUPS + 1) * GROUP)
+            by_table = work.tile([P, 2, GROUP, HEADS, SET], F32, name="by_table")
+            x = turned_ps[:].rearrange("p a (h u j) -> p a h u j", h=HEADS, u=2)
+            for table, parts, x_read in ((COS, cos_parts, x), (SIN, sin_parts, x[:, :, :, ::-1, :])):
+                nc.vector.tensor_tensor(
+                    out=by_table[:, table, :, :, :].rearrange("p a h (u j) -> p a h u j", u=2),
+                    in0=x_read,
+                    in1=parts[g // PART_GROUPS][:, rows, :]
+                    .rearrange("p a (u j) -> p a u j", u=2)
+                    .unsqueeze(2)
+                    .to_broadcast(shape),
+                    op=ALU.mult,
+                )
             return by_table
 
-        def join(engine, by_table, q_sb, mine, other, op):
+        def join(engine, by_table, q_sb):
             engine.tensor_tensor(
-                out=q_sb[:, :, :, SET + mine : SET + mine + HALF],
-                in0=by_table[:, COS, :, :, mine : mine + HALF].rearrange("p a h j -> p h a j"),
-                in1=by_table[:, SIN, :, :, other : other + HALF].rearrange("p a h j -> p h a j"),
-                op=op,
+                out=q_sb[:, :, :, SET:HEAD_DIM],
+                in0=by_table[:, COS, :, :, :].rearrange("p a h j -> p h a j"),
+                in1=by_table[:, SIN, :, :, :].rearrange("p a h j -> p h a j"),
+                op=ALU.add,
             )
 
         def store(g):
@@ -260,9 +250,7 @@ def tile_gptossmlaattention_pb_t_kernel(
                 )
 
         def rotate_and_store(g, turned_ps, q_sb):
-            by_table = multiply_tables(g, turned_ps)
-            join(nc.gpsimd, by_table, q_sb, 0, HALF, ALU.subtract)
-            join(nc.gpsimd, by_table, q_sb, HALF, 0, ALU.add)
+            join(nc.gpsimd, multiply_tables(g, turned_ps), q_sb)
             store(g)
 
         sort_by_set(bias_row[:], bias_in[:])
@@ -278,17 +266,16 @@ def tile_gptossmlaattention_pb_t_kernel(
                 turned_ps = flip_back(turned_ts[i - 2])
             plain_ps, turned_ts[i - 1] = project(packed[i - 1][0], packed[i - 1][1])
             if (i - 1) % PART_GROUPS == 0 and i > 1:
-                swap_sin((i - 1) // PART_GROUPS, nc.scalar.copy)
+                nc.scalar.mul(
+                    out=sin_low((i - 1) // PART_GROUPS), in_=sin_low((i - 1) // PART_GROUPS), mul=-1.0
+                )
             if i < GROUPS:
                 packed[i] = quantise(grouped)
-                fill_plain(plain_ps, results[i - 1])
+            fill_plain(plain_ps, results[i - 1])
             if i == 1:
-                swap_sin(0, nc.vector.tensor_copy)
+                nc.vector.tensor_scalar_mul(out=sin_low(0), in0=sin_low(0), scalar1=-1.0)
             if i >= 2:
                 rotate_and_store(i - 2, turned_ps, results[i - 2])
         last = GROUPS - 1
-        by_table = multiply_tables(last, flip_back(turned_ts[last]))
-        join(nc.gpsimd, by_table, results[last], 0, HALF, ALU.subtract)
-        fill_plain(plain_ps, results[last])
-        join(nc.vector, by_table, results[last], HALF, 0, ALU.add)
+        join(nc.vector, multiply_tables(last, flip_back(turned_ts[last])), results[last])
         store(last)

@@ -26,16 +26,19 @@ PLAIN = 0
 TURNED = 1
 ROWS = TOKENS // P
 GROUP = 4
-GROUPS = ROWS // GROUP
+GROUP_ROWS = 15 * (GROUP,) + (2, 2)
+GROUPS = len(GROUP_ROWS)
 BANK_ROWS = 2
 TABLE_PART = 16
-PART_GROUPS = TABLE_PART // GROUP
 COS = 0
 SIN = 1
 WORDS = HID // 2
 ONES = 32
-LOADED_ALONE = 4
-STORED_ALONE = 4
+HEAD_LOADS = ((0, 2), (2, 2), (4, 2), (6, 2), (8, 4), (12, 4))
+LOAD_ROWS = 8
+WEIGHT_BEHIND_ROW = 6
+STORED_IN_PAIRS = 12
+ALL_BY_FEATURE = (GROUPS - 3, GROUPS - 2, GROUPS - 1)
 
 FLOPS = 2 * TOKENS * HID * FEATURES
 
@@ -44,6 +47,8 @@ def tile_gptossmlaattention_pb_t_kernel(
     tc, hidden_states, cos, sin, Wq_words, Wq_scales, bq, out
 ):
     nc = tc.nc
+    FIRST_ROW = [sum(GROUP_ROWS[:g]) for g in range(GROUPS)]
+    LOADS = list(HEAD_LOADS) + [(row, LOAD_ROWS) for row in range(16, ROWS, LOAD_ROWS)]
     x_dram = hidden_states[0].rearrange("(p n) k -> p n k", p=P)
     cos_dram = cos[0].rearrange("(p n) j -> p n j", p=P)
     sin_dram = sin[0].rearrange("(p n) j -> p n j", p=P)
@@ -66,27 +71,23 @@ def tile_gptossmlaattention_pb_t_kernel(
         nc.vector.memset(bias_in[:], 0.0)
         nc.scalar.dma_start(out=bias_in[0:1, :], in_=bq.rearrange("(o f) -> o f", o=1))
 
-        x_tiles = []
+        x_rows = []
         cos_parts = []
         sin_parts = []
-        for g in range(GROUPS):
-            together = 1 if g < LOADED_ALONE else 2
-            if g % together == 0:
-                x_sb = const.tile([P, together * GROUP, HID], BF16, name="x%d" % g)
-                nc.sync.dma_start(
-                    out=x_sb[:], in_=x_dram[:, g * GROUP : (g + together) * GROUP, :]
-                )
-                for c in range(together):
-                    x_tiles.append(x_sb[:, c * GROUP : (c + 1) * GROUP, :])
-            if g == 1:
+        for first, count in LOADS:
+            x_sb = const.tile([P, count, HID], BF16, name="x%d" % first)
+            nc.sync.dma_start(out=x_sb[:], in_=x_dram[:, first : first + count, :])
+            for a in range(count):
+                x_rows.append(x_sb[:, a, :])
+            if first == WEIGHT_BEHIND_ROW:
                 nc.sync.dma_start(out=w_words_in[:].bitcast(I32), in_=Wq_words[0].bitcast(I32))
                 for quad in range(4):
                     nc.sync.dma_start(
                         out=w_plane_in[32 * quad : 32 * quad + 4, :].bitcast(I32),
                         in_=Wq_scales[0, 4 * quad : 4 * quad + 4, :].bitcast(I32),
                     )
-            if (g * GROUP) % TABLE_PART == 2 * GROUP:
-                part = slice((g - 2) * GROUP, (g - 2) * GROUP + TABLE_PART)
+            if first <= len(sin_parts) * TABLE_PART + 2 * GROUP < first + count:
+                part = slice(len(sin_parts) * TABLE_PART, (len(sin_parts) + 1) * TABLE_PART)
                 sin_sb = const.tile([P, TABLE_PART, SET], BF16, name="sin%d" % len(sin_parts))
                 cos_sb = const.tile([P, TABLE_PART, SET], BF16, name="cos%d" % len(cos_parts))
                 nc.sync.dma_start(out=sin_sb[:], in_=sin_dram[:, part, :])
@@ -97,12 +98,15 @@ def tile_gptossmlaattention_pb_t_kernel(
         results = []
         stores = {}
         for g in range(GROUPS):
-            together = 2 if g < GROUPS - STORED_ALONE else 1
+            together = 2 if g < STORED_IN_PAIRS else 1
             if g % together == 0:
-                q_tile = const.tile([P, HEADS, together * GROUP, HEAD_DIM], F32, name="q%d" % g)
-                for c in range(together):
-                    results.append(q_tile[:, :, c * GROUP : (c + 1) * GROUP, :])
-                stores[g + together - 1] = (g, q_tile)
+                count = sum(GROUP_ROWS[g : g + together])
+                q_tile = const.tile([P, HEADS, count, HEAD_DIM], F32, name="q%d" % g)
+                for c in range(g, g + together):
+                    at = FIRST_ROW[c] - FIRST_ROW[g]
+                    results.append(q_tile[:, :, at : at + GROUP_ROWS[c], :])
+                if g < GROUPS - 1:
+                    stores[g + together - 1] = (FIRST_ROW[g], count, q_tile)
 
         ident = const.tile([P, P], F32)
         make_identity(nc, ident[:])
@@ -112,7 +116,7 @@ def tile_gptossmlaattention_pb_t_kernel(
         w_plane = const.tile([P, 2, P], U8, align_bytes=64)
         bias_row = const.tile([P, 2, P], BF16)
         plain_bias = const.tile([P, HEADS, SET], F32)
-        turned_bias = const.tile([P, 1], F32)
+        bias_columns = const.tile([P, 2], F32)
 
         def sort_by_set(sorted_, given):
             nc.vector.tensor_copy(
@@ -133,61 +137,82 @@ def tile_gptossmlaattention_pb_t_kernel(
                 start=True,
                 stop=True,
             )
-            nc.tensor.matmul(
-                out=bias_ps[:, 2, 0:ONES],
-                lhsT=bias_row[:, TURNED, :],
-                rhs=ones[:, 0:ONES],
-                start=True,
-                stop=True,
-            )
+            for which in (PLAIN, TURNED):
+                nc.tensor.matmul(
+                    out=bias_ps[:, 2 + which, 0:ONES],
+                    lhsT=bias_row[:, which, :],
+                    rhs=ones[:, 0:ONES],
+                    start=True,
+                    stop=True,
+                )
             nc.scalar.copy(
                 out=plain_bias[:], in_=bias_ps[:, PLAIN, :].rearrange("p (h j) -> p h j", h=HEADS)
             )
-            nc.scalar.copy(out=turned_bias[:], in_=bias_ps[:, 2, 0:1])
+            nc.scalar.copy(out=bias_columns[:], in_=bias_ps[:, 2:4, 0])
 
         def sin_low(part):
             return sin_parts[part][:, :, 0:HALF]
 
         def flip(g):
-            x_words = x_tiles[g].bitcast(F32)
             grouped = mx_pool.tile([P, GROUP, P, PACK], BF16, align_bytes=64, name="grouped")
             grouped_words = grouped[:].bitcast(F32)
-            for first in range(0, GROUP, BANK_ROWS):
+            for first in range(0, GROUP_ROWS[g], BANK_ROWS):
                 flipped = flipped_psum.tile([P, BANK_ROWS, 2, P], F32, name="flipped")
                 for a in range(BANK_ROWS):
+                    x_words = x_rows[FIRST_ROW[g] + first + a].bitcast(F32)
                     for u in range(2):
-                        nc.tensor.transpose(
-                            flipped[:, a, u, :], x_words[:, first + a, u:WORDS:2], ident[:]
-                        )
+                        nc.tensor.transpose(flipped[:, a, u, :], x_words[:, u:WORDS:2], ident[:])
                 nc.scalar.copy(
                     out=grouped_words[:, first : first + BANK_ROWS, :, :],
                     in_=flipped[:].rearrange("p a u r -> p a r u"),
                 )
             return grouped
 
-        def quantise(grouped):
+        def quantise(g, grouped):
+            tokens = GROUP_ROWS[g] * P
             codes = mx_pool.tile([P, GROUP * P], U32, align_bytes=64, name="codes")
             scales = mx_pool.tile([P, GROUP * P], U8, align_bytes=64, name="scales")
             nc.vector.quantize_mx(
-                out=codes[:].bitcast(FP8X4),
-                scales=scales[:],
-                in_=grouped[:].rearrange("p a r t -> p (a r t)"),
+                out=codes[:, 0:tokens].bitcast(FP8X4),
+                scales=scales[:, 0:tokens],
+                in_=grouped[:, 0 : GROUP_ROWS[g], :, :].rearrange("p a r t -> p (a r t)"),
             )
-            return codes, scales
+            return codes[:, 0:tokens], scales[:, 0:tokens]
 
-        def project(codes, scales):
-            turned_t_ps = turned_t_psum.tile([P, GROUP * P], F32, name="turned_t_ps")
+        def project_by_feature(codes, scales, which):
+            by_feature_ps = turned_t_psum.tile([P, GROUP * P], F32, name="turned_t_ps")
             nc.tensor.matmul_mx(
-                out=turned_t_ps[:],
-                lhsT=w_words[:, TURNED, :].bitcast(FP4X4),
-                lhsT_scale=w_plane[:, TURNED, :],
-                rhs=codes[:].bitcast(FP8X4),
-                rhs_scale=scales[:],
+                out=by_feature_ps[:, 0 : codes.shape[1]],
+                lhsT=w_words[:, which, :].bitcast(FP4X4),
+                lhsT_scale=w_plane[:, which, :],
+                rhs=codes.bitcast(FP8X4),
+                rhs_scale=scales,
                 start=True,
                 stop=True,
             )
+            return by_feature_ps[:, 0 : codes.shape[1]]
+
+        def add_bias_column(by_feature_ps, which):
+            by_feature = work.tile([P, GROUP * P], F32, name="by_feature%d" % which)
+            nc.scalar.activation(
+                out=by_feature[:, 0 : by_feature_ps.shape[1]],
+                in_=by_feature_ps,
+                func=ACT.Identity,
+                bias=bias_columns[:, which : which + 1],
+                scale=1.0,
+            )
+            return by_feature[:, 0 : by_feature_ps.shape[1]]
+
+        def project_all_by_feature(codes, scales):
+            turned_t_ps = project_by_feature(codes, scales, TURNED)
+            plain_t_ps = project_by_feature(codes, scales, PLAIN)
+            turned_t = add_bias_column(turned_t_ps, TURNED)
+            return add_bias_column(plain_t_ps, PLAIN), turned_t
+
+        def project(codes, scales):
+            turned_t_ps = project_by_feature(codes, scales, TURNED)
             plain_ps = plain_psum.tile([P, GROUP, P], F32, name="plain_ps")
-            for a in range(GROUP):
+            for a in range(codes.shape[1] // P):
                 nc.tensor.matmul_mx(
                     out=plain_ps[:, a, :],
                     lhsT=codes[:, a * P : (a + 1) * P].bitcast(FP8X4),
@@ -197,36 +222,44 @@ def tile_gptossmlaattention_pb_t_kernel(
                     start=True,
                     stop=True,
                 )
-            turned_t = work.tile([P, GROUP * P], F32, name="turned_t")
-            nc.scalar.activation(
-                out=turned_t[:], in_=turned_t_ps[:], func=ACT.Identity, bias=turned_bias[:], scale=1.0
-            )
-            return plain_ps, turned_t
+            return plain_ps[:, 0 : codes.shape[1] // P, :], add_bias_column(turned_t_ps, TURNED)
 
-        def flip_back(turned_t):
-            turned_ps = turned_psum.tile([P, GROUP, P], F32, name="turned_ps")
-            for a in range(GROUP):
-                nc.tensor.transpose(turned_ps[:, a, :], turned_t[:, a * P : (a + 1) * P], ident[:])
-            return turned_ps
+        def flip_back(by_feature, by_token_ps):
+            count = by_feature.shape[1] // P
+            for a in range(count):
+                nc.tensor.transpose(
+                    by_token_ps[:, a, :], by_feature[:, a * P : (a + 1) * P], ident[:]
+                )
+            return by_token_ps[:, 0:count, :]
+
+        def flip_turned_back(turned_t):
+            return flip_back(turned_t, turned_psum.tile([P, GROUP, P], F32, name="turned_ps"))
+
+        def flip_plain_back(plain_t, q_sb):
+            plain_ps = flip_back(plain_t, plain_psum.tile([P, GROUP, P], F32, name="plain_ps"))
+            nc.scalar.copy(
+                out=q_sb[:, :, :, 0:SET], in_=plain_ps.rearrange("p a (h j) -> p h a j", h=HEADS)
+            )
 
         def fill_plain(plain_ps, q_sb):
             nc.vector.tensor_tensor(
                 out=q_sb[:, :, :, 0:SET],
-                in0=plain_ps[:].rearrange("p a (h j) -> p h a j", h=HEADS),
-                in1=plain_bias[:].unsqueeze(2).to_broadcast([P, HEADS, GROUP, SET]),
+                in0=plain_ps.rearrange("p a (h j) -> p h a j", h=HEADS),
+                in1=plain_bias[:].unsqueeze(2).to_broadcast([P, HEADS, plain_ps.shape[1], SET]),
                 op=ALU.add,
             )
 
         def multiply_tables(g, turned_ps):
-            shape = [P, GROUP, HEADS, 2, HALF]
-            rows = slice((g % PART_GROUPS) * GROUP, (g % PART_GROUPS + 1) * GROUP)
+            count = GROUP_ROWS[g]
+            shape = [P, count, HEADS, 2, HALF]
+            rows = slice(FIRST_ROW[g] % TABLE_PART, FIRST_ROW[g] % TABLE_PART + count)
             by_table = work.tile([P, 2, GROUP, HEADS, SET], F32, name="by_table")
-            x = turned_ps[:].rearrange("p a (h u j) -> p a h u j", h=HEADS, u=2)
+            x = turned_ps.rearrange("p a (h u j) -> p a h u j", h=HEADS, u=2)
             for table, parts, x_read in ((COS, cos_parts, x), (SIN, sin_parts, x[:, :, :, ::-1, :])):
                 nc.vector.tensor_tensor(
-                    out=by_table[:, table, :, :, :].rearrange("p a h (u j) -> p a h u j", u=2),
+                    out=by_table[:, table, 0:count, :, :].rearrange("p a h (u j) -> p a h u j", u=2),
                     in0=x_read,
-                    in1=parts[g // PART_GROUPS][:, rows, :]
+                    in1=parts[FIRST_ROW[g] // TABLE_PART][:, rows, :]
                     .rearrange("p a (u j) -> p a u j", u=2)
                     .unsqueeze(2)
                     .to_broadcast(shape),
@@ -234,48 +267,61 @@ def tile_gptossmlaattention_pb_t_kernel(
                 )
             return by_table
 
-        def join(engine, by_table, q_sb):
+        def join(engine, by_table, q_sb, rows):
             engine.tensor_tensor(
-                out=q_sb[:, :, :, SET:HEAD_DIM],
-                in0=by_table[:, COS, :, :, :].rearrange("p a h j -> p h a j"),
-                in1=by_table[:, SIN, :, :, :].rearrange("p a h j -> p h a j"),
+                out=q_sb[:, :, rows, SET:HEAD_DIM],
+                in0=by_table[:, COS, rows, :, :].rearrange("p a h j -> p h a j"),
+                in1=by_table[:, SIN, rows, :, :].rearrange("p a h j -> p h a j"),
                 op=ALU.add,
             )
 
         def store(g):
             if g in stores:
-                first, q_tile = stores[g]
-                nc.sync.dma_start(
-                    out=out_dram[:, :, first * GROUP : (g + 1) * GROUP, :], in_=q_tile[:]
-                )
+                first, count, q_tile = stores[g]
+                nc.sync.dma_start(out=out_dram[:, :, first : first + count, :], in_=q_tile[:])
 
         def rotate_and_store(g, turned_ps, q_sb):
-            join(nc.gpsimd, multiply_tables(g, turned_ps), q_sb)
+            join(nc.gpsimd, multiply_tables(g, turned_ps), q_sb, slice(0, GROUP_ROWS[g]))
             store(g)
 
         sort_by_set(bias_row[:], bias_in[:])
         grouped = flip(0)
         spread_bias()
-        packed = {0: quantise(grouped)}
+        packed = {0: quantise(0, grouped)}
         sort_weight()
         turned_ts = {}
+        plain_ts = {}
         for i in range(1, GROUPS + 1):
             if i < GROUPS:
                 grouped = flip(i)
             if i >= 2:
-                turned_ps = flip_back(turned_ts[i - 2])
-            plain_ps, turned_ts[i - 1] = project(packed[i - 1][0], packed[i - 1][1])
-            if (i - 1) % PART_GROUPS == 0 and i > 1:
-                nc.scalar.mul(
-                    out=sin_low((i - 1) // PART_GROUPS), in_=sin_low((i - 1) // PART_GROUPS), mul=-1.0
+                turned_ps = flip_turned_back(turned_ts[i - 2])
+            if i - 1 in ALL_BY_FEATURE:
+                plain_ts[i - 1], turned_ts[i - 1] = project_all_by_feature(
+                    packed[i - 1][0], packed[i - 1][1]
                 )
+            else:
+                plain_ps, turned_ts[i - 1] = project(packed[i - 1][0], packed[i - 1][1])
+            if i - 2 in ALL_BY_FEATURE:
+                flip_plain_back(plain_ts[i - 2], results[i - 2])
+            if FIRST_ROW[i - 1] % TABLE_PART == 0 and i > 1:
+                part = FIRST_ROW[i - 1] // TABLE_PART
+                nc.scalar.mul(out=sin_low(part), in_=sin_low(part), mul=-1.0)
             if i < GROUPS:
-                packed[i] = quantise(grouped)
-            fill_plain(plain_ps, results[i - 1])
+                packed[i] = quantise(i, grouped)
+            if i - 1 not in ALL_BY_FEATURE:
+                fill_plain(plain_ps, results[i - 1])
             if i == 1:
                 nc.vector.tensor_scalar_mul(out=sin_low(0), in0=sin_low(0), scalar1=-1.0)
             if i >= 2:
                 rotate_and_store(i - 2, turned_ps, results[i - 2])
         last = GROUPS - 1
-        join(nc.vector, multiply_tables(last, flip_back(turned_ts[last])), results[last])
-        store(last)
+        turned_ps = flip_turned_back(turned_ts[last])
+        flip_plain_back(plain_ts[last], results[last])
+        by_table = multiply_tables(last, turned_ps)
+        for a in range(GROUP_ROWS[last]):
+            join(nc.vector, by_table, results[last], slice(a, a + 1))
+            nc.sync.dma_start(
+                out=out_dram[:, :, FIRST_ROW[last] + a : FIRST_ROW[last] + a + 1, :],
+                in_=results[last][:, :, a : a + 1, :],
+            )

from contextlib import ExitStack

import concourse.mybir as mybir
from concourse.masks import make_identity

F32 = mybir.dt.float32
BF16 = mybir.dt.bfloat16
I32 = mybir.dt.int32
U32 = mybir.dt.uint32
U8 = mybir.dt.uint8
FP8X4 = mybir.dt.float8_e4m3fn_x4
FP4X4 = mybir.dt.float4_e2m1fn_x4
ALU = mybir.AluOpType
ACT = mybir.ActivationFunctionType

P = 128
PACK = 4
TOKENS = 8192
HID = 512
HEADS = 2
HEAD_DIM = 128
SET = 64
HALF = SET // 2
FEATURES = HEADS * HEAD_DIM
PLAIN = 0
TURNED = 1
ROWS = TOKENS // P
GROUP = 4
GROUP_ROWS = 15 * (GROUP,) + (2, 2)
GROUPS = len(GROUP_ROWS)
BANK_ROWS = 2
TABLE_PART = 16
COS = 0
SIN = 1
WORDS = HID // 2
ONES = 32
HEAD_LOADS = ((0, 2), (2, 2), (4, 2), (6, 2), (8, 4), (12, 4))
LOAD_ROWS = 8
WEIGHT_BEHIND_ROW = 6
STORED_IN_PAIRS = 12
ALL_BY_FEATURE = (GROUPS - 3, GROUPS - 2, GROUPS - 1)

FLOPS = 2 * TOKENS * HID * FEATURES


def tile_gptossmlaattention_pb_t_kernel(
    tc, hidden_states, cos, sin, Wq_words, Wq_scales, bq, out
):
    nc = tc.nc
    FIRST_ROW = [sum(GROUP_ROWS[:g]) for g in range(GROUPS)]
    LOADS = list(HEAD_LOADS) + [(row, LOAD_ROWS) for row in range(16, ROWS, LOAD_ROWS)]
    x_dram = hidden_states[0].rearrange("(p n) k -> p n k", p=P)
    cos_dram = cos[0].rearrange("(p n) j -> p n j", p=P)
    sin_dram = sin[0].rearrange("(p n) j -> p n j", p=P)
    out_dram = out[0].rearrange("h (p n) d -> p h n d", p=P)

    with ExitStack() as pools:
        const = pools.enter_context(tc.tile_pool(name="const", bufs=1))
        mx_pool = pools.enter_context(tc.tile_pool(name="mx", bufs=3))
        work = pools.enter_context(tc.tile_pool(name="work", bufs=3))
        flipped_psum = pools.enter_context(tc.psum_pool(name="flipped", bufs=2))
        plain_psum = pools.enter_context(tc.psum_pool(name="plain", bufs=2))
        turned_t_psum = pools.enter_context(tc.psum_pool(name="turned_t", bufs=2))
        turned_psum = pools.enter_context(tc.psum_pool(name="turned", bufs=2))
        pools.enter_context(tc.manual_schedule())

        w_words_in = const.tile([P, 2 * FEATURES], U8)
        w_plane_in = const.tile([P, FEATURES], U8)
        bias_in = const.tile([P, FEATURES], BF16)
        nc.vector.memset(w_plane_in[:].bitcast(I32), 0)
        nc.vector.memset(bias_in[:], 0.0)
        nc.scalar.dma_start(out=bias_in[0:1, :], in_=bq.rearrange("(o f) -> o f", o=1))

        x_rows = []
        cos_parts = []
        sin_parts = []
        for first, count in LOADS:
            x_sb = const.tile([P, count, HID], BF16, name="x%d" % first)
            nc.sync.dma_start(out=x_sb[:], in_=x_dram[:, first : first + count, :])
            for a in range(count):
                x_rows.append(x_sb[:, a, :])
            if first == WEIGHT_BEHIND_ROW:
                nc.sync.dma_start(out=w_words_in[:].bitcast(I32), in_=Wq_words[0].bitcast(I32))
                for quad in range(4):
                    nc.sync.dma_start(
                        out=w_plane_in[32 * quad : 32 * quad + 4, :].bitcast(I32),
                        in_=Wq_scales[0, 4 * quad : 4 * quad + 4, :].bitcast(I32),
                    )
            if first <= len(sin_parts) * TABLE_PART + 2 * GROUP < first + count:
                part = slice(len(sin_parts) * TABLE_PART, (len(sin_parts) + 1) * TABLE_PART)
                sin_sb = const.tile([P, TABLE_PART, SET], BF16, name="sin%d" % len(sin_parts))
                cos_sb = const.tile([P, TABLE_PART, SET], BF16, name="cos%d" % len(cos_parts))
                nc.sync.dma_start(out=sin_sb[:], in_=sin_dram[:, part, :])
                nc.sync.dma_start(out=cos_sb[:], in_=cos_dram[:, part, :])
                sin_parts.append(sin_sb)
                cos_parts.append(cos_sb)

        results = []
        stores = {}
        for g in range(GROUPS):
            together = 2 if g < STORED_IN_PAIRS else 1
            if g % together == 0:
                count = sum(GROUP_ROWS[g : g + together])
                q_tile = const.tile([P, HEADS, count, HEAD_DIM], F32, name="q%d" % g)
                for c in range(g, g + together):
                    at = FIRST_ROW[c] - FIRST_ROW[g]
                    results.append(q_tile[:, :, at : at + GROUP_ROWS[c], :])
                if g < GROUPS - 1:
                    stores[g + together - 1] = (FIRST_ROW[g], count, q_tile)

        ident = const.tile([P, P], F32)
        make_identity(nc, ident[:])
        ones = const.tile([P, P], BF16)
        nc.vector.memset(ones[:], 1.0)
        w_words = const.tile([P, 2, 2 * P], U8, align_bytes=64)
        w_plane = const.tile([P, 2, P], U8, align_bytes=64)
        bias_row = const.tile([P, 2, P], BF16)
        plain_bias = const.tile([P, HEADS, SET], F32)
        bias_columns = const.tile([P, 2], F32)

        def sort_by_set(sorted_, given):
            nc.vector.tensor_copy(
                out=sorted_.rearrange("p s (h b) -> p s h b", h=HEADS),
                in_=given.rearrange("p (h s b) -> p s h b", h=HEADS, s=2),
            )

        def sort_weight():
            sort_by_set(w_words[:].bitcast(I32), w_words_in[:].bitcast(I32))
            sort_by_set(w_plane[:].bitcast(I32), w_plane_in[:].bitcast(I32))

        def spread_bias():
            bias_ps = plain_psum.tile([P, GROUP, P], F32, name="plain_ps")
            nc.tensor.matmul(
                out=bias_ps[:, 0:2, :].rearrange("p s f -> p (s f)"),
                lhsT=ones[:],
                rhs=bias_row[:].rearrange("p s f -> p (s f)"),
                start=True,
                stop=True,
            )
            for which in (PLAIN, TURNED):
                nc.tensor.matmul(
                    out=bias_ps[:, 2 + which, 0:ONES],
                    lhsT=bias_row[:, which, :],
                    rhs=ones[:, 0:ONES],
                    start=True,
                    stop=True,
                )
            nc.scalar.copy(
                out=plain_bias[:], in_=bias_ps[:, PLAIN, :].rearrange("p (h j) -> p h j", h=HEADS)
            )
            nc.scalar.copy(out=bias_columns[:], in_=bias_ps[:, 2:4, 0])

        def sin_low(part):
            return sin_parts[part][:, :, 0:HALF]

        def flip(g):
            grouped = mx_pool.tile([P, GROUP, P, PACK], BF16, align_bytes=64, name="grouped")
            grouped_words = grouped[:].bitcast(F32)
            for first in range(0, GROUP_ROWS[g], BANK_ROWS):
                flipped = flipped_psum.tile([P, BANK_ROWS, 2, P], F32, name="flipped")
                for a in range(BANK_ROWS):
                    x_words = x_rows[FIRST_ROW[g] + first + a].bitcast(F32)
                    for u in range(2):
                        nc.tensor.transpose(flipped[:, a, u, :], x_words[:, u:WORDS:2], ident[:])
                nc.scalar.copy(
                    out=grouped_words[:, first : first + BANK_ROWS, :, :],
                    in_=flipped[:].rearrange("p a u r -> p a r u"),
                )
            return grouped

        def quantise(g, grouped):
            tokens = GROUP_ROWS[g] * P
            codes = mx_pool.tile([P, GROUP * P], U32, align_bytes=64, name="codes")
            scales = mx_pool.tile([P, GROUP * P], U8, align_bytes=64, name="scales")
            nc.vector.quantize_mx(
                out=codes[:, 0:tokens].bitcast(FP8X4),
                scales=scales[:, 0:tokens],
                in_=grouped[:, 0 : GROUP_ROWS[g], :, :].rearrange("p a r t -> p (a r t)"),
            )
            return codes[:, 0:tokens], scales[:, 0:tokens]

        def project_by_feature(codes, scales, which):
            by_feature_ps = turned_t_psum.tile([P, GROUP * P], F32, name="turned_t_ps")
            nc.tensor.matmul_mx(
                out=by_feature_ps[:, 0 : codes.shape[1]],
                lhsT=w_words[:, which, :].bitcast(FP4X4),
                lhsT_scale=w_plane[:, which, :],
                rhs=codes.bitcast(FP8X4),
                rhs_scale=scales,
                start=True,
                stop=True,
            )
            return by_feature_ps[:, 0 : codes.shape[1]]

        def add_bias_column(by_feature_ps, which):
            by_feature = work.tile([P, GROUP * P], F32, name="by_feature%d" % which)
            nc.scalar.activation(
                out=by_feature[:, 0 : by_feature_ps.shape[1]],
                in_=by_feature_ps,
                func=ACT.Identity,
                bias=bias_columns[:, which : which + 1],
                scale=1.0,
            )
            return by_feature[:, 0 : by_feature_ps.shape[1]]

        def project_all_by_feature(codes, scales):
            turned_t_ps = project_by_feature(codes, scales, TURNED)
            plain_t_ps = project_by_feature(codes, scales, PLAIN)
            turned_t = add_bias_column(turned_t_ps, TURNED)
            return add_bias_column(plain_t_ps, PLAIN), turned_t

        def project(codes, scales):
            turned_t_ps = project_by_feature(codes, scales, TURNED)
            plain_ps = plain_psum.tile([P, GROUP, P], F32, name="plain_ps")
            for a in range(codes.shape[1] // P):
                nc.tensor.matmul_mx(
                    out=plain_ps[:, a, :],
                    lhsT=codes[:, a * P : (a + 1) * P].bitcast(FP8X4),
                    lhsT_scale=scales[:, a * P : (a + 1) * P],
                    rhs=w_words[:, PLAIN, :].bitcast(FP4X4),
                    rhs_scale=w_plane[:, PLAIN, :],
                    start=True,
                    stop=True,
                )
            return plain_ps[:, 0 : codes.shape[1] // P, :], add_bias_column(turned_t_ps, TURNED)

        def flip_back(by_feature, by_token_ps):
            count = by_feature.shape[1] // P
            for a in range(count):
                nc.tensor.transpose(
                    by_token_ps[:, a, :], by_feature[:, a * P : (a + 1) * P], ident[:]
                )
            return by_token_ps[:, 0:count, :]

        def flip_turned_back(turned_t):
            return flip_back(turned_t, turned_psum.tile([P, GROUP, P], F32, name="turned_ps"))

        def flip_plain_back(plain_t, q_sb):
            plain_ps = flip_back(plain_t, plain_psum.tile([P, GROUP, P], F32, name="plain_ps"))
            nc.scalar.copy(
                out=q_sb[:, :, :, 0:SET], in_=plain_ps.rearrange("p a (h j) -> p h a j", h=HEADS)
            )

        def fill_plain(plain_ps, q_sb):
            nc.vector.tensor_tensor(
                out=q_sb[:, :, :, 0:SET],
                in0=plain_ps.rearrange("p a (h j) -> p h a j", h=HEADS),
                in1=plain_bias[:].unsqueeze(2).to_broadcast([P, HEADS, plain_ps.shape[1], SET]),
                op=ALU.add,
            )

        def multiply_tables(g, turned_ps):
            count = GROUP_ROWS[g]
            shape = [P, count, HEADS, 2, HALF]
            rows = slice(FIRST_ROW[g] % TABLE_PART, FIRST_ROW[g] % TABLE_PART + count)
            by_table = work.tile([P, 2, GROUP, HEADS, SET], F32, name="by_table")
            x = turned_ps.rearrange("p a (h u j) -> p a h u j", h=HEADS, u=2)
            for table, parts, x_read in ((COS, cos_parts, x), (SIN, sin_parts, x[:, :, :, ::-1, :])):
                nc.vector.tensor_tensor(
                    out=by_table[:, table, 0:count, :, :].rearrange("p a h (u j) -> p a h u j", u=2),
                    in0=x_read,
                    in1=parts[FIRST_ROW[g] // TABLE_PART][:, rows, :]
                    .rearrange("p a (u j) -> p a u j", u=2)
                    .unsqueeze(2)
                    .to_broadcast(shape),
                    op=ALU.mult,
                )
            return by_table

        def join(engine, by_table, q_sb, rows):
            engine.tensor_tensor(
                out=q_sb[:, :, rows, SET:HEAD_DIM],
                in0=by_table[:, COS, rows, :, :].rearrange("p a h j -> p h a j"),
                in1=by_table[:, SIN, rows, :, :].rearrange("p a h j -> p h a j"),
                op=ALU.add,
            )

        def store(g):
            if g in stores:
                first, count, q_tile = stores[g]
                nc.sync.dma_start(out=out_dram[:, :, first : first + count, :], in_=q_tile[:])

        def rotate_and_store(g, turned_ps, q_sb):
            join(nc.gpsimd, multiply_tables(g, turned_ps), q_sb, slice(0, GROUP_ROWS[g]))
            store(g)

        sort_by_set(bias_row[:], bias_in[:])
        grouped = flip(0)
        spread_bias()
        packed = {0: quantise(0, grouped)}
        sort_weight()
        turned_ts = {}
        plain_ts = {}
        for i in range(1, GROUPS + 1):
            if i < GROUPS:
                grouped = flip(i)
            if i >= 2:
                turned_ps = flip_turned_back(turned_ts[i - 2])
            if i - 1 in ALL_BY_FEATURE:
                plain_ts[i - 1], turned_ts[i - 1] = project_all_by_feature(
                    packed[i - 1][0], packed[i - 1][1]
                )
            else:
                plain_ps, turned_ts[i - 1] = project(packed[i - 1][0], packed[i - 1][1])
            if i - 2 in ALL_BY_FEATURE:
                flip_plain_back(plain_ts[i - 2], results[i - 2])
            if FIRST_ROW[i - 1] % TABLE_PART == 0 and i > 1:
                part = FIRST_ROW[i - 1] // TABLE_PART
                nc.scalar.mul(out=sin_low(part), in_=sin_low(part), mul=-1.0)
            if i < GROUPS:
                packed[i] = quantise(i, grouped)
            if i - 1 not in ALL_BY_FEATURE:
                fill_plain(plain_ps, results[i - 1])
            if i == 1:
                nc.vector.tensor_scalar_mul(out=sin_low(0), in0=sin_low(0), scalar1=-1.0)
            if i >= 2:
                rotate_and_store(i - 2, turned_ps, results[i - 2])
        last = GROUPS - 1
        turned_ps = flip_turned_back(turned_ts[last])
        flip_plain_back(plain_ts[last], results[last])
        by_table = multiply_tables(last, turned_ps)
        for a in range(GROUP_ROWS[last]):
            join(nc.vector, by_table, results[last], slice(a, a + 1))
            nc.sync.dma_start(
                out=out_dram[:, :, FIRST_ROW[last] + a : FIRST_ROW[last] + a + 1, :],
                in_=results[last][:, :, a : a + 1, :],
            )
